import numpy as np
import ml_dtypes


def mxq(x, axis, fmt="e4m3"):
    dtype, down = {"e4m3": (ml_dtypes.float8_e4m3fn, 7), "e5m2": (ml_dtypes.float8_e5m2, 14)}[fmt]
    v = np.moveaxis(np.asarray(x, np.float32).astype(ml_dtypes.bfloat16).astype(np.float64), axis, -1)
    blocks = v.reshape(v.shape[:-1] + (-1, 32))
    amax = np.abs(blocks).max(-1, keepdims=True)
    byte = np.maximum(np.where(amax > 0, np.frexp(amax)[1] - 1 + 127, 0) - down, 1)
    scale = np.exp2(byte - 127.0)
    codes = (blocks / scale).astype(np.float32).astype(dtype).astype(np.float64)
    return np.moveaxis((codes * scale).reshape(v.shape), -1, axis)


WIDE = False


def mx_kscale(k):
    if not WIDE:
        return np.ones(k)
    levels = np.array([10, -10, 5, -5, 0])
    if k % 512:
        return np.exp2(np.random.permutation(np.resize(levels, k // 32))).repeat(32)
    a = np.empty((k // 512, 16))
    for p in range(k // 512):
        a[p, :8] = np.random.permutation(np.resize(levels, 8))
        for g in range(8):
            far = levels[np.abs(levels - a[p, g]) >= 10]
            a[p, g + 8] = far[np.random.randint(len(far))]
    return np.exp2(a.ravel()).repeat(32)


BF16 = ml_dtypes.bfloat16


def bf(x):
    return np.asarray(x, np.float32).astype(BF16)


def f64(x):
    return np.asarray(x).astype(np.float64)


B, R, C, O, I = 1024, 8, 16, 16, 1024
EPS = 1e-8
ROUTING_ITERS = 3


def squash(s):
    norm = np.sqrt((s * s).sum(axis=-1, keepdims=True))
    return norm / (1.0 + norm * norm + EPS) * s


def softmax(b, axis):
    e = np.exp(b - b.max(axis=axis, keepdims=True))
    return e / e.sum(axis=axis, keepdims=True)


def setup_inputs():
    s = mx_kscale(I)
    return {"x": bf(np.random.standard_normal((B, R, I)) * s),
            "W": bf(np.random.standard_normal((R, C, O, I)) * (C / np.sqrt(R * O * I)) / s),
            "bias": bf(np.random.standard_normal((1, 1, C, O)) * 0.4 / np.sqrt(O))}


def reference(x, W, bias):
    xq = mxq(f64(x), 2, "e4m3")
    Wq = mxq(f64(W), 3, "e4m3")
    bias = f64(bias)
    u = xq.transpose(1, 0, 2) @ Wq.reshape(R, C * O, I).transpose(0, 2, 1)
    u_hat = u.transpose(1, 0, 2).reshape(B, R, C, O)
    b_ij = np.zeros((B, R, C, 1))
    v_j = None
    for itr in range(ROUTING_ITERS):
        c_ij = softmax(b_ij, 2)
        s_j = (c_ij * u_hat).sum(axis=1, keepdims=True) + bias
        v_j = squash(s_j)
        if itr < ROUTING_ITERS - 1:
            a_ij = (u_hat * v_j).sum(axis=-1, keepdims=True)
            b_ij = b_ij + a_ij
    return v_j[:, 0]

@@ -1,0 +1,420 @@
+from contextlib import ExitStack
+
+import concourse.mybir as mybir
+from concourse.masks import make_identity
+
+F32 = mybir.dt.float32
+BF16 = mybir.dt.bfloat16
+U32 = mybir.dt.uint32
+U8 = mybir.dt.uint8
+FP8X4 = mybir.dt.float8_e4m3fn_x4
+ALU = mybir.AluOpType
+ACT = mybir.ActivationFunctionType
+AX = mybir.AxisListType
+
+FLOPS = 2 * 1024 * 8 * 256 * 1024
+
+P = 128
+NU = 4
+EPS = 1e-8
+
+MANUAL = False
+RATE = 1
+X_EVAC = "SSSS"
+W_EVAC = "SS"
+S_MULT = "VVVV"
+REG_EVERY = 0
+SH_BUFS = 5
+LG_BUFS = 3
+BIG_BUFS = 6
+A_RED_V = ()
+
+
+def tile_capsulelayer_t_kernel(tc, x, W, bias, out):
+    nc = tc.nc
+    with ExitStack() as ctx:
+        const = ctx.enter_context(tc.tile_pool(name="const", bufs=1))
+        big = ctx.enter_context(tc.tile_pool(name="big", bufs=BIG_BUFS))
+        xq_pool = ctx.enter_context(tc.tile_pool(name="xq", bufs=2))
+        u_pool = ctx.enter_context(tc.tile_pool(name="u", bufs=4))
+        un = ctx.enter_context(tc.tile_pool(name="un", bufs=4))
+        ps_sh = ctx.enter_context(tc.psum_pool(name="pssh", bufs=SH_BUFS))
+        ps_lg = ctx.enter_context(tc.psum_pool(name="pslg", bufs=LG_BUFS))
+
+        def copy_on(letter, dst, src):
+            if letter == "S":
+                nc.scalar.copy(out=dst, in_=src)
+            else:
+                nc.vector.tensor_copy(out=dst, in_=src)
+
+        ident = const.tile([P, P], F32, name="ident")
+        make_identity(nc, ident[:])
+        tinyb = const.tile([P, 1], F32, name="tinyb")
+        nc.vector.memset(tinyb[:], 1e-30)
+        braw = const.tile([P, 256], BF16, name="braw")
+        nc.sync.dma_start(out=braw[:], in_=bias.rearrange("a b c o -> (a b c o)").partition_broadcast(P))
+        bc = const.tile([P, 256], F32, name="bc")
+        nc.vector.tensor_copy(
+            out=bc[:].rearrange("p (o c) -> p o c", c=16),
+            in_=braw[:].rearrange("p (c o) -> p o c", o=16),
+        )
+        wc = const.tile([P, 8, 512], U32, name="wc", align_bytes=64)
+        ws = const.tile([P, 8, 512], U8, name="ws", align_bytes=64)
+        bias_t = const.tile([P, 2], F32, name="bias_t")
+        tpb = ps_sh.tile([P, 4, P], F32, tag="sh", name="tpb")
+        for h in range(2):
+            nc.tensor.transpose(out=tpb[:, h, :], in_=bc[:, h * P:(h + 1) * P], identity=ident[:])
+        for h in range(2):
+            nc.vector.tensor_copy(out=bias_t[:, h:h + 1], in_=tpb[:, h, 0:1])
+
+        if MANUAL:
+            ctx.enter_context(tc.manual_schedule())
+
+        w_rows = W.rearrange("r c o i -> (r c o) i")
+        fe = dict()
+        st = [dict() for q in range(NU)]
+
+        def load_w(wt):
+            win = big.tile([P, 8192], BF16, tag="big", name="win", align_bytes=64)
+            nc.sync.dma_start(
+                out=win[:].rearrange("p (t i) -> p t i", t=8),
+                in_=w_rows[wt * 1024:(wt + 1) * 1024, :].rearrange("(t p) i -> p t i", p=P),
+            )
+            fe["w%d" % wt] = win
+
+        def w_step(wq):
+            wt, sub = divmod(wq, 2)
+            if sub == 0:
+                fe["gw%d" % wt] = big.tile([P, 8192], BF16, tag="big", name="grpw", align_bytes=64)
+            ww = fe["w%d" % wt][:].bitcast(F32)
+            grp = fe["gw%d" % wt]
+            gv = grp[:].bitcast(F32).rearrange("p (r g o c u) -> p r g o c u", r=4, g=2, o=16, c=16, u=2)
+            for rl in range(2 * sub, 2 * sub + 2):
+                for h in range(2):
+                    t = rl * 2 + h
+                    tp = ps_sh.tile([P, 4, P], F32, tag="sh", name="tpw")
+                    for k in range(4):
+                        nc.tensor.transpose(
+                            out=tp[:, k, :], in_=ww[:, t * 512 + (k // 2) * 256 + k % 2: t * 512 + (k // 2 + 1) * 256: 2], identity=ident[:]
+                        )
+                    for g in range(2):
+                        copy_on(
+                            W_EVAC[g],
+                            gv[:, rl, g, :, 8 * h:8 * h + 8, :],
+                            tp[:, 2 * g:2 * g + 2, :].rearrange("p u (c o) -> p o c u", o=16),
+                        )
+            nc.vector.quantize_mx(
+                out=wc[:, 2 * wq:2 * wq + 2, :].rearrange("p a b -> p (a b)").bitcast(FP8X4),
+                scales=ws[:, 2 * wq:2 * wq + 2, :].rearrange("p a b -> p (a b)"),
+                in_=grp[:, sub * 4096:(sub + 1) * 4096],
+            )
+
+        def load_x(t):
+            xin = big.tile([P, 8192], BF16, tag="big", name="xin", align_bytes=64)
+            for half in range(2):
+                nc.sync.dma_start(
+                    out=xin[:, half * 4096:(half + 1) * 4096],
+                    in_=x[t * P:(t + 1) * P, 4 * half:4 * half + 4, :].rearrange("b r i -> b (r i)"),
+                )
+            fe["x%d" % t] = xin
+
+        def fe_transposes(i, pair):
+            t, half = divmod(i, 2)
+            xw = fe["x%d" % t][:].bitcast(F32)
+            gv = fe["g%d" % t][:].bitcast(F32).rearrange("p (r g b u) -> p r g b u", r=8, g=2, b=P, u=2)
+            for rl in range(2 * pair, 2 * pair + 2):
+                r = 4 * half + rl
+                tp = ps_sh.tile([P, 4, P], F32, tag="sh", name="tpx")
+                for k in range(4):
+                    nc.tensor.transpose(
+                        out=tp[:, k, :], in_=xw[:, r * 512 + (k // 2) * 256 + k % 2: r * 512 + (k // 2 + 1) * 256: 2], identity=ident[:]
+                    )
+                copy_on(X_EVAC[rl], gv[:, r], tp[:].rearrange("p (g u) b -> p g b u", u=2))
+
+        def fe_quant(i):
+            t, half = divmod(i, 2)
+            nc.vector.quantize_mx(
+                out=fe["xc%d" % t][:, 8 * half:8 * half + 8, :].rearrange("p a b -> p (a b)").bitcast(FP8X4),
+                scales=fe["xs%d" % t][:, 8 * half:8 * half + 8, :].rearrange("p a b -> p (a b)"),
+                in_=fe["g%d" % t][:, half * 4096:(half + 1) * 4096],
+            )
+
+        def fe_mx(i, pair):
+            t, half = divmod(i, 2)
+            q, j = divmod(t, 2)
+            xc = fe["xc%d" % t]
+            xs = fe["xs%d" % t]
+            u = st[q]["u"]
+            jr = 2 * half + pair
+            ups = ps_sh.tile([P, 512], F32, tag="sh", name="ups")
+            for rr in range(2):
+                r = 2 * jr + rr
+                for g in range(2):
+                    nc.tensor.matmul_mx(
+                        out=ups[:, rr * 256:(rr + 1) * 256],
+                        lhsT=xc[:, 2 * r + g, :].bitcast(FP8X4),
+                        lhsT_scale=xs[:, 2 * r + g, :],
+                        rhs=wc[:, r, g * 256:(g + 1) * 256].bitcast(FP8X4),
+                        rhs_scale=ws[:, r, g * 256:(g + 1) * 256],
+                        start=(g == 0),
+                        stop=(g == 1),
+                    )
+            nc.scalar.copy(out=u[:, j * 2048 + jr * 512: j * 2048 + (jr + 1) * 512], in_=ups[:])
+            s1 = st[q]["s"]
+            for rr in range(2):
+                nc.vector.scalar_tensor_tensor(
+                    out=s1[:, j * 256:(j + 1) * 256], in0=ups[:, rr * 256:(rr + 1) * 256], scalar=1.0 / 16.0,
+                    in1=(bc[:] if 2 * jr + rr == 0 else s1[:, j * 256:(j + 1) * 256]), op0=ALU.mult, op1=ALU.add,
+                )
+
+        def fe_step(i):
+            t, half = divmod(i, 2)
+            if i < 16 and half == 0:
+                if t + 1 < 8:
+                    load_x(t + 1)
+                fe["g%d" % t] = big.tile([P, 8192], BF16, tag="big", name="grpx", align_bytes=64)
+                fe["xc%d" % t] = xq_pool.tile([P, 16, P], U32, tag="xc", name="xc", align_bytes=64)
+                fe["xs%d" % t] = xq_pool.tile([P, 16, P], U8, tag="xs", name="xs", align_bytes=64)
+                if t % 2 == 0:
+                    st[t // 2]["u"] = u_pool.tile([P, 4096], F32, tag="u", name="u")
+                    st[t // 2]["s"] = un.tile([P, 512], F32, tag="s1", name="s1")
+            for pair in range(2):
+                if i < 16:
+                    fe_transposes(i, pair)
+                if i > 0:
+                    fe_mx(i - 1, pair)
+            if i < 16:
+                fe_quant(i)
+
+        count = [0]
+
+        def turn(dst, src, first, last):
+            count[0] = count[0] + 1
+            nc.tensor.matmul(
+                out=dst, lhsT=src, rhs=ident[:],
+                is_transpose=(REG_EVERY == 0 or count[0] % REG_EVERY != 0),
+                start=first, stop=last,
+            )
+
+        def acc_transposes(dst, srcs):
+            n = len(srcs)
+            for i in range(n):
+                turn(dst, srcs[i], i == 0, i == n - 1)
+
+        def s_mult(q, j):
+            d = st[q]
+            if j == 0:
+                d["p"] = big.tile([P, 4096], F32, tag="big", name="p_s", align_bytes=64)
+            pv = d["p"][:].rearrange("p (a h o c) -> p a h o c", a=16, h=2, c=16)
+            uv = d["u"][:].rearrange("p (a h o c) -> p a h o c", a=16, h=2, c=16)
+            cv = d["td"][:].rearrange("p (a c) -> p a c", c=16)
+            for h in range(2):
+                eng = nc.gpsimd if S_MULT[2 * j + h] == "G" else nc.vector
+                eng.tensor_tensor(
+                    out=pv[:, 8 * j:8 * j + 8, h],
+                    in0=uv[:, 8 * j:8 * j + 8, h],
+                    in1=cv[:, 8 * j:8 * j + 8, :].unsqueeze(2).to_broadcast([P, 8, 8, 16]),
+                    op=ALU.mult,
+                )
+
+        def s_acc(q, k, j):
+            d = st[q]
+            src = d["u"] if k == 0 else d["p"]
+            sv = src[:].rearrange("p (j r h k) -> p j r h k", j=2, r=8, h=2)
+            if j == 0:
+                d["acc"] = ps_sh.tile([P, 2, 2, P], F32, tag="sh", name="acc_s")
+            for h in range(2):
+                acc_transposes(d["acc"][:, j, h, :], [sv[:, j, r, h, :] for r in range(8)])
+
+        def s_evac(q, k):
+            d = st[q]
+            d["ta"] = un.tile([P, 512], F32, tag="ta", name="ta")
+            tv = d["ta"][:].rearrange("p (j h b) -> p j h b", j=2, h=2)
+            for h in range(2):
+                nc.scalar.activation(
+                    out=tv[:, :, h, :], in_=d["acc"][:, :, h, :], func=ACT.Identity,
+                    bias=bias_t[:, h:h + 1], scale=(1.0 / 16.0 if k == 0 else 1.0),
+                )
+
+        def s_back(q):
+            d = st[q]
+            d["s"] = ps_lg.tile([P, 512], F32, tag="lg", name="back_s")
+            for jh in range(4):
+                turn(d["s"][:, jh * P:(jh + 1) * P], d["ta"][:, jh * P:(jh + 1) * P], True, True)
+
+        def sq_square(q, k):
+            d = st[q]
+            if k == 0:
+                d["ta"] = un.tile([P, 512], F32, tag="ta", name="ta")
+            nc.scalar.activation(out=d["ta"][:], in_=d["s"][:], func=ACT.Square)
+
+        def sq_n2(q):
+            d = st[q]
+            d["n2"] = un.tile([P, 32], F32, tag="n2", name="n2")
+            nc.vector.tensor_reduce(
+                out=d["n2"][:].rearrange("p (j c) -> p j c", j=2),
+                in_=d["ta"][:].rearrange("p (j o c) -> p j c o", j=2, c=16),
+                axis=AX.X, op=ALU.add,
+            )
+            d["rd"] = un.tile([P, 32], F32, tag="rd", name="rd")
+            nc.vector.tensor_scalar(out=d["rd"][:], in0=d["n2"][:], scalar1=1.0 + EPS, scalar2=None, op0=ALU.add)
+            nc.vector.reciprocal(out=d["rd"][:], in_=d["rd"][:])
+
+        def sq_sqrt(q):
+            d = st[q]
+            d["nn"] = un.tile([P, 32], F32, tag="nn", name="nn")
+            nc.scalar.activation(out=d["nn"][:], in_=d["n2"][:], func=ACT.Sqrt, bias=tinyb[:, 0:1])
+
+        def sq_gain(q):
+            d = st[q]
+            d["gain"] = un.tile([P, 32], F32, tag="gain", name="gain")
+            nc.vector.tensor_mul(out=d["gain"][:], in0=d["nn"][:], in1=d["rd"][:])
+
+        def a_mult(q, j):
+            d = st[q]
+            if j == 0:
+                d["pa"] = big.tile([P, 4096], F32, tag="big", name="p_a", align_bytes=64)
+            pv = d["pa"][:].rearrange("p (j o r c) -> p j o r c", j=2, o=16, c=16)
+            uv = d["u"][:].rearrange("p (j r o c) -> p j o r c", j=2, r=8, c=16)
+            sv = d["s"][:].rearrange("p (j o c) -> p j o c", j=2, c=16)
+            for oh in range(2):
+                nc.vector.tensor_tensor(
+                    out=pv[:, j, 8 * oh:8 * oh + 8],
+                    in0=uv[:, j, 8 * oh:8 * oh + 8],
+                    in1=sv[:, j, 8 * oh:8 * oh + 8, :].unsqueeze(2).to_broadcast([P, 8, 8, 16]),
+                    op=ALU.mult,
+                )
+
+        def a_acc(q, k, j):
+            d = st[q]
+            if k in A_RED_V:
+                if j == 0:
+                    d["araw"] = un.tile([P, 256], F32, tag="tb", name="araw_sb")
+                nc.vector.tensor_reduce(
+                    out=d["araw"][:, j * P:(j + 1) * P],
+                    in_=d["pa"][:, j * 2048:(j + 1) * 2048].rearrange("p (o k) -> p k o", o=16),
+                    axis=AX.X, op=ALU.add,
+                )
+                return
+            pk = d["pa"][:].rearrange("p (j o k) -> p j o k", j=2, o=16)
+            if j == 0:
+                d["acca"] = ps_sh.tile([P, 2, P], F32, tag="sh", name="acc_a")
+            acc_transposes(d["acca"][:, j, :], [pk[:, j, o, :] for o in range(16)])
+
+        def a_evac(q):
+            d = st[q]
+            d["tb"] = un.tile([P, 256], F32, tag="tb", name="tb")
+            nc.scalar.copy(out=d["tb"][:].rearrange("p (j b) -> p j b", j=2), in_=d["acca"][:])
+
+        def a_back(q):
+            d = st[q]
+            d["araw"] = ps_sh.tile([P, 256], F32, tag="sh", name="back_a")
+            for j in range(2):
+                turn(d["araw"][:, j * P:(j + 1) * P], d["tb"][:, j * P:(j + 1) * P], True, True)
+
+        def a_logit(q, k):
+            d = st[q]
+            gv = d["gain"][:].rearrange("p (j c) -> p j c", j=2).unsqueeze(2).to_broadcast([P, 2, 8, 16])
+            av = d["araw"][:].rearrange("p (j r c) -> p j r c", j=2, c=16)
+            if k == 0:
+                d["logit"] = un.tile([P, 256], F32, tag="logit", name="logit")
+                nc.vector.tensor_tensor(
+                    out=d["logit"][:].rearrange("p (j r c) -> p j r c", j=2, c=16), in0=av, in1=gv, op=ALU.mult
+                )
+            else:
+                tmp = d["araw"] if k in A_RED_V else d["tb"]
+                nc.vector.tensor_tensor(
+                    out=tmp[:].rearrange("p (j r c) -> p j r c", j=2, c=16), in0=av, in1=gv, op=ALU.mult
+                )
+                nc.vector.tensor_add(out=d["logit"][:], in0=tmp[:], in1=d["logit"][:])
+            lv = d["logit"][:].rearrange("p (a c) -> p a c", c=16)
+            d["mx"] = un.tile([P, 16], F32, tag="mx", name="mx")
+            nc.vector.tensor_reduce(out=d["mx"][:], in_=lv, axis=AX.X, op=ALU.max)
+            d["td"] = un.tile([P, 256], F32, tag="td", name="td")
+            nc.vector.tensor_tensor(
+                out=d["td"][:].rearrange("p (a c) -> p a c", c=16), in0=lv,
+                in1=d["mx"][:].unsqueeze(2).to_broadcast([P, 16, 16]), op=ALU.subtract,
+            )
+
+        def a_exp(q):
+            d = st[q]
+            nc.scalar.activation(out=d["td"][:], in_=d["td"][:], func=ACT.Exp)
+
+        def a_soft(q):
+            d = st[q]
+            ev = d["td"][:].rearrange("p (a c) -> p a c", c=16)
+            nc.vector.tensor_reduce(out=d["mx"][:], in_=ev, axis=AX.X, op=ALU.add)
+            nc.vector.reciprocal(out=d["mx"][:], in_=d["mx"][:])
+            nc.vector.tensor_tensor(
+                out=ev, in0=ev, in1=d["mx"][:].unsqueeze(2).to_broadcast([P, 16, 16]), op=ALU.mult
+            )
+
+        def out_v(q):
+            d = st[q]
+            nc.vector.tensor_tensor(
+                out=d["ta"][:].rearrange("p (j c o) -> p j c o", j=2, o=16),
+                in0=d["s"][:].rearrange("p (j o c) -> p j c o", j=2, c=16),
+                in1=d["gain"][:].rearrange("p (j c) -> p j c", j=2).unsqueeze(3).to_broadcast([P, 2, 16, 16]),
+                op=ALU.mult,
+            )
+            nc.sync.dma_start(
+                out=out[q * 256:(q + 1) * 256].rearrange("(j b) c o -> b j (c o)", j=2),
+                in_=d["ta"][:].rearrange("p (j k) -> p j k", j=2),
+            )
+
+        def routing_steps(q):
+            steps = []
+            for k in range(3):
+                if k > 0:
+                    steps.append(lambda: s_mult(q, 0))
+                    steps.append(lambda: s_mult(q, 1))
+                    steps.append(lambda k=k: s_acc(q, k, 0))
+                    steps.append(lambda k=k: s_acc(q, k, 1))
+                    steps.append(lambda k=k: s_evac(q, k))
+                    steps.append(lambda: s_back(q))
+                steps.append(lambda k=k: sq_square(q, k))
+                if k < 2:
+                    steps.append(lambda: a_mult(q, 0))
+                    steps.append(lambda: sq_n2(q))
+                    steps.append(lambda: a_mult(q, 1))
+                    steps.append(lambda k=k: a_acc(q, k, 0))
+                    steps.append(lambda: sq_sqrt(q))
+                    steps.append(lambda k=k: a_acc(q, k, 1))
+                    steps.append(lambda: sq_gain(q))
+                    if k not in A_RED_V:
+                        steps.append(lambda: a_evac(q))
+                        steps.append(lambda: a_back(q))
+                    steps.append(lambda k=k: a_logit(q, k))
+                    steps.append(lambda: a_exp(q))
+                    steps.append(lambda: a_soft(q))
+                else:
+                    steps.append(lambda: sq_n2(q))
+                    steps.append(lambda: sq_sqrt(q))
+                    steps.append(lambda: sq_gain(q))
+                    steps.append(lambda: out_v(q))
+            return steps
+
+        chains = []
+
+        def advance(n):
+            for rep in range(n):
+                for ch in chains:
+                    if ch[1] < len(ch[0]):
+                        ch[0][ch[1]]()
+                        ch[1] = ch[1] + 1
+
+        load_w(0)
+        load_x(0)
+        load_w(1)
+        w_step(0)
+        w_step(1)
+        fe_step(0)
+        w_step(2)
+        w_step(3)
+        for i in range(1, 17):
+            fe_step(i)
+            if i % 4 == 0:
+                chains.append([routing_steps(i // 4 - 1), 0])
+            advance(RATE)
+        for rep in range(60):
+            advance(1)

@@ -18,16 +18,17 @@ P = 128
 NU = 4
 EPS = 1e-8
 
-MANUAL = False
-RATE = 1
-X_EVAC = "SSSS"
-W_EVAC = "SS"
-S_MULT = "VVVV"
-REG_EVERY = 0
-SH_BUFS = 5
-LG_BUFS = 3
+MANUAL = True
+S0_V = (0, 1, 2, 3)
+N2_PE = True
+X_EVAC = "SS"
+W_EVAC = "SV"
+RATE = 1.0
+SH_BUFS = 6
+LG_BUFS = 2
 BIG_BUFS = 6
-A_RED_V = ()
+MX_LAG = 3
+TAIL = 60
 
 
 def tile_capsulelayer_t_kernel(tc, x, W, bias, out):
@@ -35,7 +36,7 @@ def tile_capsulelayer_t_kernel(tc, x, W, bias, out):
     with ExitStack() as ctx:
         const = ctx.enter_context(tc.tile_pool(name="const", bufs=1))
         big = ctx.enter_context(tc.tile_pool(name="big", bufs=BIG_BUFS))
-        xq_pool = ctx.enter_context(tc.tile_pool(name="xq", bufs=2))
+        xq_pool = ctx.enter_context(tc.tile_pool(name="xq", bufs=6))
         u_pool = ctx.enter_context(tc.tile_pool(name="u", bufs=4))
         un = ctx.enter_context(tc.tile_pool(name="un", bufs=4))
         ps_sh = ctx.enter_context(tc.psum_pool(name="pssh", bufs=SH_BUFS))
@@ -51,36 +52,44 @@ def tile_capsulelayer_t_kernel(tc, x, W, bias, out):
         make_identity(nc, ident[:])
         tinyb = const.tile([P, 1], F32, name="tinyb")
         nc.vector.memset(tinyb[:], 1e-30)
-        braw = const.tile([P, 256], BF16, name="braw")
-        nc.sync.dma_start(out=braw[:], in_=bias.rearrange("a b c o -> (a b c o)").partition_broadcast(P))
-        bc = const.tile([P, 256], F32, name="bc")
-        nc.vector.tensor_copy(
-            out=bc[:].rearrange("p (o c) -> p o c", c=16),
-            in_=braw[:].rearrange("p (c o) -> p o c", o=16),
-        )
         wc = const.tile([P, 8, 512], U32, name="wc", align_bytes=64)
         ws = const.tile([P, 8, 512], U8, name="ws", align_bytes=64)
         bias_t = const.tile([P, 2], F32, name="bias_t")
-        tpb = ps_sh.tile([P, 4, P], F32, tag="sh", name="tpb")
-        for h in range(2):
-            nc.tensor.transpose(out=tpb[:, h, :], in_=bc[:, h * P:(h + 1) * P], identity=ident[:])
-        for h in range(2):
-            nc.vector.tensor_copy(out=bias_t[:, h:h + 1], in_=tpb[:, h, 0:1])
-
-        if MANUAL:
-            ctx.enter_context(tc.manual_schedule())
+        braw = const.tile([P, 256], BF16, name="braw")
+        bc = const.tile([P, 256], F32, name="bc")
+        sel = const.tile([P, 16], F32, name="sel")
 
         w_rows = W.rearrange("r c o i -> (r c o) i")
         fe = dict()
         st = [dict() for q in range(NU)]
 
-        def load_w(wt):
-            win = big.tile([P, 8192], BF16, tag="big", name="win", align_bytes=64)
-            nc.sync.dma_start(
-                out=win[:].rearrange("p (t i) -> p t i", t=8),
-                in_=w_rows[wt * 1024:(wt + 1) * 1024, :].rearrange("(t p) i -> p t i", p=P),
+        def load_w(wq):
+            if wq % 2 == 0:
+                fe["w%d" % (wq // 2)] = big.tile([P, 8192], BF16, tag="big", name="win", align_bytes=64)
+            win = fe["w%d" % (wq // 2)]
+            h = wq % 2
+            for s in range(2):
+                nc.sync.dma_start(
+                    out=win[:, h * 4096 + s * 2048:h * 4096 + (s + 1) * 2048].rearrange("p (t i) -> p t i", t=2),
+                    in_=w_rows[wq * 512 + s * 256:wq * 512 + (s + 1) * 256, :].rearrange("(t p) i -> p t i", p=P),
+                )
+
+        def load_bias():
+            nc.sync.dma_start(out=braw[:], in_=bias.rearrange("a b c o -> (a b c o)").partition_broadcast(P))
+
+        def prep_bias():
+            nc.vector.tensor_copy(
+                out=bc[:].rearrange("p (o c) -> p o c", c=16),
+                in_=braw[:].rearrange("p (c o) -> p o c", o=16),
             )
-            fe["w%d" % wt] = win
+            nc.vector.tensor_reduce(
+                out=sel[:], in_=ident[:].rearrange("p (o c) -> p c o", c=16), axis=AX.X, op=ALU.add
+            )
+            tpb = ps_sh.tile([P, 4, P], F32, tag="sh", name="tpb")
+            for h in range(2):
+                nc.tensor.transpose(out=tpb[:, h, :], in_=bc[:, h * P:(h + 1) * P], identity=ident[:])
+            for h in range(2):
+                nc.vector.tensor_copy(out=bias_t[:, h:h + 1], in_=tpb[:, h, 0:1])
 
         def w_step(wq):
             wt, sub = divmod(wq, 2)
@@ -94,107 +103,92 @@ def tile_capsulelayer_t_kernel(tc, x, W, bias, out):
                     t = rl * 2 + h
                     tp = ps_sh.tile([P, 4, P], F32, tag="sh", name="tpw")
                     for k in range(4):
-                        nc.tensor.transpose(
-                            out=tp[:, k, :], in_=ww[:, t * 512 + (k // 2) * 256 + k % 2: t * 512 + (k // 2 + 1) * 256: 2], identity=ident[:]
-                        )
+                        at = t * 512 + (k // 2) * 256 + k % 2
+                        nc.tensor.transpose(out=tp[:, k, :], in_=ww[:, at: at - k % 2 + 256: 2], identity=ident[:])
                     for g in range(2):
                         copy_on(
-                            W_EVAC[g],
+                            W_EVAC[h],
                             gv[:, rl, g, :, 8 * h:8 * h + 8, :],
                             tp[:, 2 * g:2 * g + 2, :].rearrange("p u (c o) -> p o c u", o=16),
                         )
+
+        def w_quant(wq):
+            sub = wq % 2
+            grp = fe["gw%d" % (wq // 2)]
             nc.vector.quantize_mx(
                 out=wc[:, 2 * wq:2 * wq + 2, :].rearrange("p a b -> p (a b)").bitcast(FP8X4),
                 scales=ws[:, 2 * wq:2 * wq + 2, :].rearrange("p a b -> p (a b)"),
                 in_=grp[:, sub * 4096:(sub + 1) * 4096],
             )
 
-        def load_x(t):
-            xin = big.tile([P, 8192], BF16, tag="big", name="xin", align_bytes=64)
-            for half in range(2):
-                nc.sync.dma_start(
-                    out=xin[:, half * 4096:(half + 1) * 4096],
-                    in_=x[t * P:(t + 1) * P, 4 * half:4 * half + 4, :].rearrange("b r i -> b (r i)"),
-                )
-            fe["x%d" % t] = xin
-
-        def fe_transposes(i, pair):
-            t, half = divmod(i, 2)
-            xw = fe["x%d" % t][:].bitcast(F32)
-            gv = fe["g%d" % t][:].bitcast(F32).rearrange("p (r g b u) -> p r g b u", r=8, g=2, b=P, u=2)
-            for rl in range(2 * pair, 2 * pair + 2):
-                r = 4 * half + rl
-                tp = ps_sh.tile([P, 4, P], F32, tag="sh", name="tpx")
-                for k in range(4):
-                    nc.tensor.transpose(
-                        out=tp[:, k, :], in_=xw[:, r * 512 + (k // 2) * 256 + k % 2: r * 512 + (k // 2 + 1) * 256: 2], identity=ident[:]
-                    )
-                copy_on(X_EVAC[rl], gv[:, r], tp[:].rearrange("p (g u) b -> p g b u", u=2))
-
-        def fe_quant(i):
-            t, half = divmod(i, 2)
-            nc.vector.quantize_mx(
-                out=fe["xc%d" % t][:, 8 * half:8 * half + 8, :].rearrange("p a b -> p (a b)").bitcast(FP8X4),
-                scales=fe["xs%d" % t][:, 8 * half:8 * half + 8, :].rearrange("p a b -> p (a b)"),
-                in_=fe["g%d" % t][:, half * 4096:(half + 1) * 4096],
+        def load_x(t, half):
+            if half == 0:
+                fe["x%d" % t] = big.tile([P, 8192], BF16, tag="big", name="xin", align_bytes=64)
+            nc.sync.dma_start(
+                out=fe["x%d" % t][:, half * 4096:(half + 1) * 4096],
+                in_=x[t * P:(t + 1) * P, 4 * half:4 * half + 4, :].rearrange("b r i -> b (r i)"),
             )
 
-        def fe_mx(i, pair):
-            t, half = divmod(i, 2)
+        def fe_transposes(i):
+            t, jr = divmod(i, 4)
+            if jr == 0:
+                fe["g%d" % t] = big.tile([P, 8192], BF16, tag="big", name="grpx", align_bytes=64)
+            xw = fe["x%d" % t][:].bitcast(F32)
+            gv = fe["g%d" % t][:].bitcast(F32).rearrange("p (r g b u) -> p r g b u", r=8, g=2, b=P, u=2)
+            for rr in range(2):
+                r = 2 * jr + rr
+                tp = ps_sh.tile([P, 4, P], F32, tag="sh", name="tpx")
+                for k in range(4):
+                    at = r * 512 + (k // 2) * 256 + k % 2
+                    nc.tensor.transpose(out=tp[:, k, :], in_=xw[:, at: at - k % 2 + 256: 2], identity=ident[:])
+                copy_on(X_EVAC[rr], gv[:, r], tp[:].rearrange("p (g u) b -> p g b u", u=2))
+
+        def fe_quant(i):
+            t, jr = divmod(i, 4)
+            xc = xq_pool.tile([P, 4, P], U32, tag="xc", name="xc", align_bytes=64)
+            xs = xq_pool.tile([P, 4, P], U8, tag="xs", name="xs", align_bytes=64)
+            fe["xc%d" % i] = xc
+            fe["xs%d" % i] = xs
+            nc.vector.quantize_mx(
+                out=xc[:].rearrange("p a b -> p (a b)").bitcast(FP8X4),
+                scales=xs[:].rearrange("p a b -> p (a b)"),
+                in_=fe["g%d" % t][:, jr * 2048:(jr + 1) * 2048],
+            )
+
+        def fe_mx(i):
+            t, jr = divmod(i, 4)
             q, j = divmod(t, 2)
-            xc = fe["xc%d" % t]
-            xs = fe["xs%d" % t]
+            if j == 0 and jr == 0:
+                st[q]["u"] = u_pool.tile([P, 4096], F32, tag="u", name="u")
+                if q in S0_V:
+                    st[q]["s"] = un.tile([P, 512], F32, tag="s1", name="s1")
+            xc = fe["xc%d" % i]
+            xs = fe["xs%d" % i]
             u = st[q]["u"]
-            jr = 2 * half + pair
             ups = ps_sh.tile([P, 512], F32, tag="sh", name="ups")
             for rr in range(2):
                 r = 2 * jr + rr
                 for g in range(2):
                     nc.tensor.matmul_mx(
                         out=ups[:, rr * 256:(rr + 1) * 256],
-                        lhsT=xc[:, 2 * r + g, :].bitcast(FP8X4),
-                        lhsT_scale=xs[:, 2 * r + g, :],
+                        lhsT=xc[:, 2 * rr + g, :].bitcast(FP8X4),
+                        lhsT_scale=xs[:, 2 * rr + g, :],
                         rhs=wc[:, r, g * 256:(g + 1) * 256].bitcast(FP8X4),
                         rhs_scale=ws[:, r, g * 256:(g + 1) * 256],
                         start=(g == 0),
                         stop=(g == 1),
                     )
             nc.scalar.copy(out=u[:, j * 2048 + jr * 512: j * 2048 + (jr + 1) * 512], in_=ups[:])
-            s1 = st[q]["s"]
-            for rr in range(2):
-                nc.vector.scalar_tensor_tensor(
-                    out=s1[:, j * 256:(j + 1) * 256], in0=ups[:, rr * 256:(rr + 1) * 256], scalar=1.0 / 16.0,
-                    in1=(bc[:] if 2 * jr + rr == 0 else s1[:, j * 256:(j + 1) * 256]), op0=ALU.mult, op1=ALU.add,
-                )
-
-        def fe_step(i):
-            t, half = divmod(i, 2)
-            if i < 16 and half == 0:
-                if t + 1 < 8:
-                    load_x(t + 1)
-                fe["g%d" % t] = big.tile([P, 8192], BF16, tag="big", name="grpx", align_bytes=64)
-                fe["xc%d" % t] = xq_pool.tile([P, 16, P], U32, tag="xc", name="xc", align_bytes=64)
-                fe["xs%d" % t] = xq_pool.tile([P, 16, P], U8, tag="xs", name="xs", align_bytes=64)
-                if t % 2 == 0:
-                    st[t // 2]["u"] = u_pool.tile([P, 4096], F32, tag="u", name="u")
-                    st[t // 2]["s"] = un.tile([P, 512], F32, tag="s1", name="s1")
-            for pair in range(2):
-                if i < 16:
-                    fe_transposes(i, pair)
-                if i > 0:
-                    fe_mx(i - 1, pair)
-            if i < 16:
-                fe_quant(i)
-
-        count = [0]
+            if q in S0_V:
+                s1 = st[q]["s"]
+                for rr in range(2):
+                    nc.vector.scalar_tensor_tensor(
+                        out=s1[:, j * 256:(j + 1) * 256], in0=ups[:, rr * 256:(rr + 1) * 256], scalar=1.0 / 16.0,
+                        in1=(bc[:] if 2 * jr + rr == 0 else s1[:, j * 256:(j + 1) * 256]), op0=ALU.mult, op1=ALU.add,
+                    )
 
         def turn(dst, src, first, last):
-            count[0] = count[0] + 1
-            nc.tensor.matmul(
-                out=dst, lhsT=src, rhs=ident[:],
-                is_transpose=(REG_EVERY == 0 or count[0] % REG_EVERY != 0),
-                start=first, stop=last,
-            )
+            nc.tensor.matmul(out=dst, lhsT=src, rhs=ident[:], is_transpose=True, start=first, stop=last)
 
         def acc_transposes(dst, srcs):
             n = len(srcs)
@@ -209,8 +203,7 @@ def tile_capsulelayer_t_kernel(tc, x, W, bias, out):
             uv = d["u"][:].rearrange("p (a h o c) -> p a h o c", a=16, h=2, c=16)
             cv = d["td"][:].rearrange("p (a c) -> p a c", c=16)
             for h in range(2):
-                eng = nc.gpsimd if S_MULT[2 * j + h] == "G" else nc.vector
-                eng.tensor_tensor(
+                nc.vector.tensor_tensor(
                     out=pv[:, 8 * j:8 * j + 8, h],
                     in0=uv[:, 8 * j:8 * j + 8, h],
                     in1=cv[:, 8 * j:8 * j + 8, :].unsqueeze(2).to_broadcast([P, 8, 8, 16]),
@@ -242,31 +235,42 @@ def tile_capsulelayer_t_kernel(tc, x, W, bias, out):
             for jh in range(4):
                 turn(d["s"][:, jh * P:(jh + 1) * P], d["ta"][:, jh * P:(jh + 1) * P], True, True)
 
+        def n2_pe(q, k):
+            return N2_PE and (k > 0 or q not in S0_V)
+
         def sq_square(q, k):
             d = st[q]
-            if k == 0:
-                d["ta"] = un.tile([P, 512], F32, tag="ta", name="ta")
-            nc.scalar.activation(out=d["ta"][:], in_=d["s"][:], func=ACT.Square)
+            d["sq"] = un.tile([P, 512], F32, tag="sq", name="sq")
+            src = d["ta"] if n2_pe(q, k) else d["s"]
+            nc.scalar.activation(out=d["sq"][:], in_=src[:], func=ACT.Square)
 
-        def sq_n2(q):
+        def sq_n2(q, k):
             d = st[q]
-            d["n2"] = un.tile([P, 32], F32, tag="n2", name="n2")
-            nc.vector.tensor_reduce(
-                out=d["n2"][:].rearrange("p (j c) -> p j c", j=2),
-                in_=d["ta"][:].rearrange("p (j o c) -> p j c o", j=2, c=16),
-                axis=AX.X, op=ALU.add,
-            )
+            if n2_pe(q, k):
+                d["n2"] = ps_sh.tile([P, 32], F32, tag="sh", name="n2p")
+                for jh in range(4):
+                    nc.tensor.matmul(
+                        out=d["n2"][:, (jh // 2) * 16:(jh // 2) * 16 + 16], lhsT=d["sq"][:, jh * P:(jh + 1) * P],
+                        rhs=sel[:], start=(jh % 2 == 0), stop=(jh % 2 == 1),
+                    )
+            else:
+                d["n2"] = un.tile([P, 32], F32, tag="n2", name="n2")
+                nc.vector.tensor_reduce(
+                    out=d["n2"][:].rearrange("p (j c) -> p j c", j=2),
+                    in_=d["sq"][:].rearrange("p (j o c) -> p j c o", j=2, c=16),
+                    axis=AX.X, op=ALU.add,
+                )
+
+        def sq_rd(q):
+            d = st[q]
             d["rd"] = un.tile([P, 32], F32, tag="rd", name="rd")
             nc.vector.tensor_scalar(out=d["rd"][:], in0=d["n2"][:], scalar1=1.0 + EPS, scalar2=None, op0=ALU.add)
-            nc.vector.reciprocal(out=d["rd"][:], in_=d["rd"][:])
-
-        def sq_sqrt(q):
-            d = st[q]
             d["nn"] = un.tile([P, 32], F32, tag="nn", name="nn")
             nc.scalar.activation(out=d["nn"][:], in_=d["n2"][:], func=ACT.Sqrt, bias=tinyb[:, 0:1])
 
         def sq_gain(q):
             d = st[q]
+            nc.vector.reciprocal(out=d["rd"][:], in_=d["rd"][:])
             d["gain"] = un.tile([P, 32], F32, tag="gain", name="gain")
             nc.vector.tensor_mul(out=d["gain"][:], in0=d["nn"][:], in1=d["rd"][:])
 
@@ -285,17 +289,8 @@ def tile_capsulelayer_t_kernel(tc, x, W, bias, out):
                     op=ALU.mult,
                 )
 
-        def a_acc(q, k, j):
+        def a_acc(q, j):
             d = st[q]
-            if k in A_RED_V:
-                if j == 0:
-                    d["araw"] = un.tile([P, 256], F32, tag="tb", name="araw_sb")
-                nc.vector.tensor_reduce(
-                    out=d["araw"][:, j * P:(j + 1) * P],
-                    in_=d["pa"][:, j * 2048:(j + 1) * 2048].rearrange("p (o k) -> p k o", o=16),
-                    axis=AX.X, op=ALU.add,
-                )
-                return
             pk = d["pa"][:].rearrange("p (j o k) -> p j o k", j=2, o=16)
             if j == 0:
                 d["acca"] = ps_sh.tile([P, 2, P], F32, tag="sh", name="acc_a")
@@ -322,7 +317,7 @@ def tile_capsulelayer_t_kernel(tc, x, W, bias, out):
                     out=d["logit"][:].rearrange("p (j r c) -> p j r c", j=2, c=16), in0=av, in1=gv, op=ALU.mult
                 )
             else:
-                tmp = d["araw"] if k in A_RED_V else d["tb"]
+                tmp = d["tb"]
                 nc.vector.tensor_tensor(
                     out=tmp[:].rearrange("p (j r c) -> p j r c", j=2, c=16), in0=av, in1=gv, op=ALU.mult
                 )
@@ -369,27 +364,29 @@ def tile_capsulelayer_t_kernel(tc, x, W, bias, out):
                     steps.append(lambda: s_mult(q, 0))
                     steps.append(lambda: s_mult(q, 1))
                     steps.append(lambda k=k: s_acc(q, k, 0))
+                if k > 0 or q not in S0_V:
+                    if k == 0:
+                        steps.append(lambda k=k: s_acc(q, k, 0))
                     steps.append(lambda k=k: s_acc(q, k, 1))
                     steps.append(lambda k=k: s_evac(q, k))
                     steps.append(lambda: s_back(q))
                 steps.append(lambda k=k: sq_square(q, k))
                 if k < 2:
                     steps.append(lambda: a_mult(q, 0))
-                    steps.append(lambda: sq_n2(q))
+                    steps.append(lambda k=k: sq_n2(q, k))
                     steps.append(lambda: a_mult(q, 1))
-                    steps.append(lambda k=k: a_acc(q, k, 0))
-                    steps.append(lambda: sq_sqrt(q))
-                    steps.append(lambda k=k: a_acc(q, k, 1))
+                    steps.append(lambda: a_acc(q, 0))
+                    steps.append(lambda: sq_rd(q))
+                    steps.append(lambda: a_acc(q, 1))
                     steps.append(lambda: sq_gain(q))
-                    if k not in A_RED_V:
-                        steps.append(lambda: a_evac(q))
-                        steps.append(lambda: a_back(q))
+                    steps.append(lambda: a_evac(q))
+                    steps.append(lambda: a_back(q))
                     steps.append(lambda k=k: a_logit(q, k))
                     steps.append(lambda: a_exp(q))
                     steps.append(lambda: a_soft(q))
                 else:
-                    steps.append(lambda: sq_n2(q))
-                    steps.append(lambda: sq_sqrt(q))
+                    steps.append(lambda k=k: sq_n2(q, k))
+                    steps.append(lambda: sq_rd(q))
                     steps.append(lambda: sq_gain(q))
                     steps.append(lambda: out_v(q))
             return steps
@@ -404,17 +401,38 @@ def tile_capsulelayer_t_kernel(tc, x, W, bias, out):
                         ch[1] = ch[1] + 1
 
         load_w(0)
-        load_x(0)
+        load_x(0, 0)
         load_w(1)
-        w_step(0)
-        w_step(1)
-        fe_step(0)
-        w_step(2)
-        w_step(3)
-        for i in range(1, 17):
-            fe_step(i)
-            if i % 4 == 0:
-                chains.append([routing_steps(i // 4 - 1), 0])
-            advance(RATE)
-        for rep in range(60):
+        load_x(0, 1)
+        load_w(2)
+        load_bias()
+        load_w(3)
+        load_x(1, 0)
+        load_x(1, 1)
+        if MANUAL:
+            ctx.enter_context(tc.manual_schedule())
+        owed = 0.0
+        for i in range(32 + MX_LAG):
+            if i < 32:
+                if i % 4 == 0 and 2 <= i // 4 + 1 < 8:
+                    load_x(i // 4 + 1, 0)
+                    load_x(i // 4 + 1, 1)
+                if i < 4:
+                    w_step(i)
+                if i == 2:
+                    prep_bias()
+                fe_transposes(i)
+            if i < 4:
+                w_quant(i)
+            if 0 <= i - 1 < 32:
+                fe_quant(i - 1)
+            if i >= MX_LAG:
+                fe_mx(i - MX_LAG)
+                if (i - MX_LAG) % 8 == 7:
+                    chains.append([routing_steps((i - MX_LAG) // 8), 0])
+            owed = owed + (RATE if i < 32 else 1.0)
+            while owed >= 1.0:
+                owed = owed - 1.0
+                advance(1)
+        for rep in range(TAIL):
             advance(1)

@@ -19,15 +19,28 @@ NU = 4
 EPS = 1e-8
 
 MANUAL = True
-S0_V = (0, 1, 2, 3)
+EARLY_V = 0
+START = 0
+S_CUT = 1
+A_CUT = 1
+OLD_FIRST = False
+ORDER = "AMTQ"
+FUSE_EB = False
+FUSE_ACC = False
+FUSE_SM = False
+LATE_RATE = 1.0
+QUANT2 = True
+PLAIN = 0
+RD_S = True
+S0_V = (0, 1)
 N2_PE = True
 X_EVAC = "SS"
-W_EVAC = "SV"
-RATE = 1.0
+W_EVAC = "SS"
+RATE = 0.5
 SH_BUFS = 6
 LG_BUFS = 2
 BIG_BUFS = 6
-MX_LAG = 3
+MX_LAG = 4
 TAIL = 60
 
 
@@ -36,7 +49,7 @@ def tile_capsulelayer_t_kernel(tc, x, W, bias, out):
     with ExitStack() as ctx:
         const = ctx.enter_context(tc.tile_pool(name="const", bufs=1))
         big = ctx.enter_context(tc.tile_pool(name="big", bufs=BIG_BUFS))
-        xq_pool = ctx.enter_context(tc.tile_pool(name="xq", bufs=6))
+        xq_pool = ctx.enter_context(tc.tile_pool(name="xq", bufs=3))
         u_pool = ctx.enter_context(tc.tile_pool(name="u", bufs=4))
         un = ctx.enter_context(tc.tile_pool(name="un", bufs=4))
         ps_sh = ctx.enter_context(tc.psum_pool(name="pssh", bufs=SH_BUFS))
@@ -141,18 +154,20 @@ def tile_capsulelayer_t_kernel(tc, x, W, bias, out):
                 for k in range(4):
                     at = r * 512 + (k // 2) * 256 + k % 2
                     nc.tensor.transpose(out=tp[:, k, :], in_=xw[:, at: at - k % 2 + 256: 2], identity=ident[:])
-                copy_on(X_EVAC[rr], gv[:, r], tp[:].rearrange("p (g u) b -> p g b u", u=2))
+                copy_on("V" if rr == 1 and i < EARLY_V else X_EVAC[rr], gv[:, r], tp[:].rearrange("p (g u) b -> p g b u", u=2))
 
         def fe_quant(i):
             t, jr = divmod(i, 4)
-            xc = xq_pool.tile([P, 4, P], U32, tag="xc", name="xc", align_bytes=64)
-            xs = xq_pool.tile([P, 4, P], U8, tag="xs", name="xs", align_bytes=64)
-            fe["xc%d" % i] = xc
-            fe["xs%d" % i] = xs
+            if jr % 2 == 0:
+                return
+            xc = xq_pool.tile([P, 8, P], U32, tag="xc", name="xc", align_bytes=64)
+            xs = xq_pool.tile([P, 8, P], U8, tag="xs", name="xs", align_bytes=64)
+            fe["xc%d" % (i // 2)] = xc
+            fe["xs%d" % (i // 2)] = xs
             nc.vector.quantize_mx(
                 out=xc[:].rearrange("p a b -> p (a b)").bitcast(FP8X4),
                 scales=xs[:].rearrange("p a b -> p (a b)"),
-                in_=fe["g%d" % t][:, jr * 2048:(jr + 1) * 2048],
+                in_=fe["g%d" % t][:, (jr - 1) * 2048:(jr + 1) * 2048],
             )
 
         def fe_mx(i):
@@ -162,8 +177,9 @@ def tile_capsulelayer_t_kernel(tc, x, W, bias, out):
                 st[q]["u"] = u_pool.tile([P, 4096], F32, tag="u", name="u")
                 if q in S0_V:
                     st[q]["s"] = un.tile([P, 512], F32, tag="s1", name="s1")
-            xc = fe["xc%d" % i]
-            xs = fe["xs%d" % i]
+            xc = fe["xc%d" % (i // 2)]
+            xs = fe["xs%d" % (i // 2)]
+            rb = 4 * (jr % 2)
             u = st[q]["u"]
             ups = ps_sh.tile([P, 512], F32, tag="sh", name="ups")
             for rr in range(2):
@@ -171,8 +187,8 @@ def tile_capsulelayer_t_kernel(tc, x, W, bias, out):
                 for g in range(2):
                     nc.tensor.matmul_mx(
                         out=ups[:, rr * 256:(rr + 1) * 256],
-                        lhsT=xc[:, 2 * rr + g, :].bitcast(FP8X4),
-                        lhsT_scale=xs[:, 2 * rr + g, :],
+                        lhsT=xc[:, rb + 2 * rr + g, :].bitcast(FP8X4),
+                        lhsT_scale=xs[:, rb + 2 * rr + g, :],
                         rhs=wc[:, r, g * 256:(g + 1) * 256].bitcast(FP8X4),
                         rhs_scale=ws[:, r, g * 256:(g + 1) * 256],
                         start=(g == 0),
@@ -187,8 +203,12 @@ def tile_capsulelayer_t_kernel(tc, x, W, bias, out):
                         in1=(bc[:] if 2 * jr + rr == 0 else s1[:, j * 256:(j + 1) * 256]), op0=ALU.mult, op1=ALU.add,
                     )
 
+        turns = [0]
+
         def turn(dst, src, first, last):
-            nc.tensor.matmul(out=dst, lhsT=src, rhs=ident[:], is_transpose=True, start=first, stop=last)
+            turns[0] = turns[0] + 1
+            plain = PLAIN > 0 and turns[0] % PLAIN == 0
+            nc.tensor.matmul(out=dst, lhsT=src, rhs=ident[:], is_transpose=not plain, start=first, stop=last)
 
         def acc_transposes(dst, srcs):
             n = len(srcs)
@@ -199,15 +219,14 @@ def tile_capsulelayer_t_kernel(tc, x, W, bias, out):
             d = st[q]
             if j == 0:
                 d["p"] = big.tile([P, 4096], F32, tag="big", name="p_s", align_bytes=64)
-            pv = d["p"][:].rearrange("p (a h o c) -> p a h o c", a=16, h=2, c=16)
-            uv = d["u"][:].rearrange("p (a h o c) -> p a h o c", a=16, h=2, c=16)
+            pv = d["p"][:].rearrange("p (a o c) -> p a o c", a=16, c=16)
+            uv = d["u"][:].rearrange("p (a o c) -> p a o c", a=16, c=16)
             cv = d["td"][:].rearrange("p (a c) -> p a c", c=16)
-            for h in range(2):
+            w = 16 // S_CUT
+            for o in range(0, 16, w):
                 nc.vector.tensor_tensor(
-                    out=pv[:, 8 * j:8 * j + 8, h],
-                    in0=uv[:, 8 * j:8 * j + 8, h],
-                    in1=cv[:, 8 * j:8 * j + 8, :].unsqueeze(2).to_broadcast([P, 8, 8, 16]),
-                    op=ALU.mult,
+                    out=pv[:, 8 * j:8 * j + 8, o:o + w], in0=uv[:, 8 * j:8 * j + 8, o:o + w],
+                    in1=cv[:, 8 * j:8 * j + 8, :].unsqueeze(2).to_broadcast([P, 8, w, 16]), op=ALU.mult,
                 )
 
         def s_acc(q, k, j):
@@ -264,7 +283,10 @@ def tile_capsulelayer_t_kernel(tc, x, W, bias, out):
         def sq_rd(q):
             d = st[q]
             d["rd"] = un.tile([P, 32], F32, tag="rd", name="rd")
-            nc.vector.tensor_scalar(out=d["rd"][:], in0=d["n2"][:], scalar1=1.0 + EPS, scalar2=None, op0=ALU.add)
+            if RD_S:
+                nc.scalar.activation(out=d["rd"][:], in_=d["n2"][:], func=ACT.Identity, bias=1.0 + EPS)
+            else:
+                nc.vector.tensor_scalar(out=d["rd"][:], in0=d["n2"][:], scalar1=1.0 + EPS, scalar2=None, op0=ALU.add)
             d["nn"] = un.tile([P, 32], F32, tag="nn", name="nn")
             nc.scalar.activation(out=d["nn"][:], in_=d["n2"][:], func=ACT.Sqrt, bias=tinyb[:, 0:1])
 
@@ -281,12 +303,11 @@ def tile_capsulelayer_t_kernel(tc, x, W, bias, out):
             pv = d["pa"][:].rearrange("p (j o r c) -> p j o r c", j=2, o=16, c=16)
             uv = d["u"][:].rearrange("p (j r o c) -> p j o r c", j=2, r=8, c=16)
             sv = d["s"][:].rearrange("p (j o c) -> p j o c", j=2, c=16)
-            for oh in range(2):
+            w = 16 // A_CUT
+            for o in range(0, 16, w):
                 nc.vector.tensor_tensor(
-                    out=pv[:, j, 8 * oh:8 * oh + 8],
-                    in0=uv[:, j, 8 * oh:8 * oh + 8],
-                    in1=sv[:, j, 8 * oh:8 * oh + 8, :].unsqueeze(2).to_broadcast([P, 8, 8, 16]),
-                    op=ALU.mult,
+                    out=pv[:, j, o:o + w], in0=uv[:, j, o:o + w],
+                    in1=sv[:, j, o:o + w].unsqueeze(2).to_broadcast([P, w, 8, 16]), op=ALU.mult,
                 )
 
         def a_acc(q, j):
@@ -360,42 +381,51 @@ def tile_capsulelayer_t_kernel(tc, x, W, bias, out):
         def routing_steps(q):
             steps = []
             for k in range(3):
+                def add(*fs):
+                    for f in fs:
+                        steps.append(f)
+
+                def both(f, g):
+                    return lambda: (f(), g())
+
                 if k > 0:
-                    steps.append(lambda: s_mult(q, 0))
-                    steps.append(lambda: s_mult(q, 1))
-                    steps.append(lambda k=k: s_acc(q, k, 0))
+                    if FUSE_SM:
+                        add(both(lambda: s_mult(q, 0), lambda: s_mult(q, 1)))
+                    else:
+                        add(lambda: s_mult(q, 0), lambda: s_mult(q, 1))
                 if k > 0 or q not in S0_V:
-                    if k == 0:
-                        steps.append(lambda k=k: s_acc(q, k, 0))
-                    steps.append(lambda k=k: s_acc(q, k, 1))
-                    steps.append(lambda k=k: s_evac(q, k))
-                    steps.append(lambda: s_back(q))
-                steps.append(lambda k=k: sq_square(q, k))
+                    if FUSE_ACC:
+                        add(both(lambda k=k: s_acc(q, k, 0), lambda k=k: s_acc(q, k, 1)))
+                    else:
+                        add(lambda k=k: s_acc(q, k, 0), lambda k=k: s_acc(q, k, 1))
+                    if FUSE_EB:
+                        add(both(lambda k=k: s_evac(q, k), lambda: s_back(q)))
+                    else:
+                        add(lambda k=k: s_evac(q, k), lambda: s_back(q))
+                add(lambda k=k: sq_square(q, k))
                 if k < 2:
-                    steps.append(lambda: a_mult(q, 0))
-                    steps.append(lambda k=k: sq_n2(q, k))
-                    steps.append(lambda: a_mult(q, 1))
-                    steps.append(lambda: a_acc(q, 0))
-                    steps.append(lambda: sq_rd(q))
-                    steps.append(lambda: a_acc(q, 1))
-                    steps.append(lambda: sq_gain(q))
-                    steps.append(lambda: a_evac(q))
-                    steps.append(lambda: a_back(q))
-                    steps.append(lambda k=k: a_logit(q, k))
-                    steps.append(lambda: a_exp(q))
-                    steps.append(lambda: a_soft(q))
+                    if FUSE_SM:
+                        add(both(lambda: a_mult(q, 0), lambda: a_mult(q, 1)), lambda k=k: sq_n2(q, k))
+                    else:
+                        add(lambda: a_mult(q, 0), lambda k=k: sq_n2(q, k), lambda: a_mult(q, 1))
+                    if FUSE_ACC:
+                        add(both(lambda: a_acc(q, 0), lambda: a_acc(q, 1)), lambda: sq_rd(q), lambda: sq_gain(q))
+                    else:
+                        add(lambda: a_acc(q, 0), lambda: sq_rd(q), lambda: a_acc(q, 1), lambda: sq_gain(q))
+                    if FUSE_EB:
+                        add(both(lambda: a_evac(q), lambda: a_back(q)))
+                    else:
+                        add(lambda: a_evac(q), lambda: a_back(q))
+                    add(lambda k=k: a_logit(q, k), lambda: a_exp(q), lambda: a_soft(q))
                 else:
-                    steps.append(lambda k=k: sq_n2(q, k))
-                    steps.append(lambda: sq_rd(q))
-                    steps.append(lambda: sq_gain(q))
-                    steps.append(lambda: out_v(q))
+                    add(lambda k=k: sq_n2(q, k), lambda: sq_rd(q), lambda: sq_gain(q), lambda: out_v(q))
             return steps
 
         chains = []
 
         def advance(n):
             for rep in range(n):
-                for ch in chains:
+                for ch in (chains if OLD_FIRST else chains[::-1]):
                     if ch[1] < len(ch[0]):
                         ch[0][ch[1]]()
                         ch[1] = ch[1] + 1
@@ -411,28 +441,37 @@ def tile_capsulelayer_t_kernel(tc, x, W, bias, out):
         load_x(1, 1)
         if MANUAL:
             ctx.enter_context(tc.manual_schedule())
-        owed = 0.0
-        for i in range(32 + MX_LAG):
-            if i < 32:
-                if i % 4 == 0 and 2 <= i // 4 + 1 < 8:
-                    load_x(i // 4 + 1, 0)
-                    load_x(i // 4 + 1, 1)
-                if i < 4:
-                    w_step(i)
-                if i == 2:
-                    prep_bias()
-                fe_transposes(i)
-            if i < 4:
-                w_quant(i)
-            if 0 <= i - 1 < 32:
-                fe_quant(i - 1)
-            if i >= MX_LAG:
-                fe_mx(i - MX_LAG)
-                if (i - MX_LAG) % 8 == 7:
-                    chains.append([routing_steps((i - MX_LAG) // 8), 0])
-            owed = owed + (RATE if i < 32 else 1.0)
-            while owed >= 1.0:
-                owed = owed - 1.0
+        owed = [0.0]
+
+        def pace(i):
+            owed[0] = owed[0] + (RATE if i < 32 else LATE_RATE)
+            while owed[0] >= 1.0:
+                owed[0] = owed[0] - 1.0
                 advance(1)
+
+        for i in range(32 + MX_LAG):
+            for o in ORDER:
+                if o == "T" and i < 32:
+                    if i % 4 == 0 and 2 <= i // 4 + 1 < 8:
+                        load_x(i // 4 + 1, 0)
+                        load_x(i // 4 + 1, 1)
+                    if i < 4:
+                        w_step(i)
+                    if i == 2:
+                        prep_bias()
+                    fe_transposes(i)
+                if o == "Q":
+                    if i < 4:
+                        w_quant(i)
+                    if 0 <= i - 1 < 32:
+                        fe_quant(i - 1)
+                if o == "M" and i >= MX_LAG:
+                    fe_mx(i - MX_LAG)
+                    if (i - MX_LAG) % 8 == 7:
+                        chains.append([routing_steps((i - MX_LAG) // 8), 0])
+                        if len(chains) == 1:
+                            advance(START)
+                if o == "A":
+                    pace(i)
         for rep in range(TAIL):
             advance(1)

@@ -24,7 +24,7 @@ START = 0
 S_CUT = 1
 A_CUT = 1
 OLD_FIRST = False
-ORDER = "AMTQ"
+ORDER = "MATQ"
 FUSE_EB = False
 FUSE_ACC = False
 FUSE_SM = False
@@ -36,11 +36,11 @@ S0_V = (0, 1)
 N2_PE = True
 X_EVAC = "SS"
 W_EVAC = "SS"
-RATE = 0.5
+RATE = 0.75
 SH_BUFS = 6
 LG_BUFS = 2
 BIG_BUFS = 6
-MX_LAG = 4
+MX_LAG = 7
 TAIL = 60
 
 

@@ -15,33 +15,44 @@ AX = mybir.AxisListType
 FLOPS = 2 * 1024 * 8 * 256 * 1024
 
 P = 128
-NU = 4
+UNITS = ((0,1,),(2,3,),(4,5,),(6,7,),)
 EPS = 1e-8
 
 MANUAL = True
 EARLY_V = 0
-START = 0
 S_CUT = 1
 A_CUT = 1
-OLD_FIRST = False
-ORDER = "MATQ"
-FUSE_EB = False
-FUSE_ACC = False
-FUSE_SM = False
+OLD_FIRST = True
+ORDER = 'AMTQ'
 LATE_RATE = 1.0
 QUANT2 = True
 PLAIN = 0
 RD_S = True
-S0_V = (0, 1)
+S0_V = (0,1,)
 N2_PE = True
-X_EVAC = "SS"
-W_EVAC = "SS"
+X_EVAC = 'SS'
+W_EVAC = 'SS'
 RATE = 0.75
-SH_BUFS = 6
-LG_BUFS = 2
+SH_BUFS = 5
+LG_BUFS = 3
 BIG_BUFS = 6
-MX_LAG = 7
+MX_LAG = 6
 TAIL = 60
+MXS0 = ()
+G_R = 3
+G_O = 4
+C_PS = True
+G_SUB = True
+G_NORM = True
+G_ADD = False
+G_SQ = False
+G_FROM = 0
+S0_BUFS = 1
+SB_PLAIN = False
+AB_PLAIN = False
+HA = 0
+HS = 0
+CP_BUFS = 1
 
 
 def tile_capsulelayer_t_kernel(tc, x, W, bias, out):
@@ -50,10 +61,11 @@ def tile_capsulelayer_t_kernel(tc, x, W, bias, out):
         const = ctx.enter_context(tc.tile_pool(name="const", bufs=1))
         big = ctx.enter_context(tc.tile_pool(name="big", bufs=BIG_BUFS))
         xq_pool = ctx.enter_context(tc.tile_pool(name="xq", bufs=3))
-        u_pool = ctx.enter_context(tc.tile_pool(name="u", bufs=4))
+        u_pool = ctx.enter_context(tc.tile_pool(name="u", bufs=1))
         un = ctx.enter_context(tc.tile_pool(name="un", bufs=4))
         ps_sh = ctx.enter_context(tc.psum_pool(name="pssh", bufs=SH_BUFS))
         ps_lg = ctx.enter_context(tc.psum_pool(name="pslg", bufs=LG_BUFS))
+        ps_s0 = ctx.enter_context(tc.psum_pool(name="pss0", bufs=S0_BUFS)) if len(MXS0) > 0 else None
 
         def copy_on(letter, dst, src):
             if letter == "S":
@@ -74,7 +86,12 @@ def tile_capsulelayer_t_kernel(tc, x, W, bias, out):
 
         w_rows = W.rearrange("r c o i -> (r c o) i")
         fe = dict()
-        st = [dict() for q in range(NU)]
+        st = [dict() for q in UNITS]
+        unit_of = dict()
+        for q in range(len(UNITS)):
+            for j in range(len(UNITS[q])):
+                unit_of[UNITS[q][j]] = (q, j)
+            st[q]["nj"] = len(UNITS[q])
 
         def load_w(wq):
             if wq % 2 == 0:
@@ -172,11 +189,13 @@ def tile_capsulelayer_t_kernel(tc, x, W, bias, out):
 
         def fe_mx(i):
             t, jr = divmod(i, 4)
-            q, j = divmod(t, 2)
+            q, j = unit_of[t]
             if j == 0 and jr == 0:
-                st[q]["u"] = u_pool.tile([P, 4096], F32, tag="u", name="u")
-                if q in S0_V:
-                    st[q]["s"] = un.tile([P, 512], F32, tag="s1", name="s1")
+                st[q]["u"] = u_pool.tile([P, 2048 * st[q]["nj"]], F32, tag="u%d" % q, name="u")
+                if q in MXS0:
+                    st[q]["s0"] = ps_s0.tile([P, 256 * st[q]["nj"]], F32, tag="s0", name="s0")
+                if q in S0_V or q in MXS0:
+                    st[q]["s"] = un.tile([P, 256 * st[q]["nj"]], F32, tag="s1", name="s1")
             xc = fe["xc%d" % (i // 2)]
             xs = fe["xs%d" % (i // 2)]
             rb = 4 * (jr % 2)
@@ -194,6 +213,19 @@ def tile_capsulelayer_t_kernel(tc, x, W, bias, out):
                         start=(g == 0),
                         stop=(g == 1),
                     )
+            if q in MXS0:
+                for rr in range(2):
+                    r = 2 * jr + rr
+                    for g in range(2):
+                        nc.tensor.matmul_mx(
+                            out=st[q]["s0"][:, j * 256:(j + 1) * 256],
+                            lhsT=xc[:, rb + 2 * rr + g, :].bitcast(FP8X4),
+                            lhsT_scale=xs[:, rb + 2 * rr + g, :],
+                            rhs=wc[:, r, g * 256:(g + 1) * 256].bitcast(FP8X4),
+                            rhs_scale=ws[:, r, g * 256:(g + 1) * 256],
+                            start=(r == 0 and g == 0),
+                            stop=(r == 7 and g == 1),
+                        )
             nc.scalar.copy(out=u[:, j * 2048 + jr * 512: j * 2048 + (jr + 1) * 512], in_=ups[:])
             if q in S0_V:
                 s1 = st[q]["s"]
@@ -203,11 +235,71 @@ def tile_capsulelayer_t_kernel(tc, x, W, bias, out):
                         in1=(bc[:] if 2 * jr + rr == 0 else s1[:, j * 256:(j + 1) * 256]), op0=ALU.mult, op1=ALU.add,
                     )
 
+        def s0_bias(q):
+            d = st[q]
+            nc.vector.scalar_tensor_tensor(
+                out=d["s"][:].rearrange("p (j k) -> p j k", k=256), in0=d["s0"][:].rearrange("p (j k) -> p j k", k=256),
+                scalar=1.0 / 16.0, in1=bc[:].unsqueeze(1).to_broadcast([P, d["nj"], 256]), op0=ALU.mult, op1=ALU.add,
+            )
+
+        def gr(q):
+            return G_R if q >= G_FROM else 0
+
+        def go(q, k):
+            return G_O if q >= G_FROM and (k > 0 or not (q in S0_V or q in MXS0)) else 0
+
+        def c_copy(q):
+            d = st[q]
+            d["cp"] = ps_lg.tile([P, P * d["nj"]], F32, tag="lg", name="cp")
+            nc.tensor.matmul(out=d["cp"][:], lhsT=ident[:], rhs=d["td"][:], start=True, stop=True)
+
+        def s_mult_g(q, j):
+            d = st[q]
+            n = gr(q)
+            if j == 0:
+                d["p"] = big.tile([P, 2048 * d["nj"]], F32, tag="big", name="p_s", align_bytes=64)
+            pv = d["p"][:].rearrange("p (a o c) -> p a o c", o=16, c=16)
+            uv = d["u"][:].rearrange("p (a o c) -> p a o c", o=16, c=16)
+            cv = d["td"][:].rearrange("p (a c) -> p a c", c=16)
+            nc.gpsimd.tensor_tensor(
+                out=pv[:, 8 * j + 8 - n:8 * j + 8], in0=uv[:, 8 * j + 8 - n:8 * j + 8],
+                in1=cv[:, 8 * j + 8 - n:8 * j + 8, :].unsqueeze(2).to_broadcast([P, n, 16, 16]), op=ALU.mult,
+            )
+
+        def s_copy(q):
+            d = st[q]
+            n = G_O
+            d["sg"] = un.tile([P, 16 * n * d["nj"]], F32, tag="sg", name="sg")
+            nc.scalar.copy(
+                out=d["sg"][:].rearrange("p (j k) -> p j k", k=16 * n),
+                in_=d["s"][:].rearrange("p (j k) -> p j k", k=256)[:, :, 256 - 16 * n:],
+            )
+
+        def a_half(q, j):
+            pk = st[q]["pa"][:].rearrange("p (j o k) -> p j o k", o=16, k=P)
+            nc.gpsimd.tensor_tensor(out=pk[:, j, 0:HA], in0=pk[:, j, 0:HA], in1=pk[:, j, 16 - HA:16], op=ALU.add)
+
+        def s_half(q, j):
+            pk = st[q]["p"][:].rearrange("p (j r k) -> p j r k", r=8, k=256)
+            nc.gpsimd.tensor_tensor(out=pk[:, j, 0:HS], in0=pk[:, j, 0:HS], in1=pk[:, j, 8 - HS:8], op=ALU.add)
+
+        def a_mult_g(q, j):
+            d = st[q]
+            n = G_O
+            if j == 0:
+                d["pa"] = big.tile([P, 2048 * d["nj"]], F32, tag="big", name="p_a", align_bytes=64)
+            pv = d["pa"][:].rearrange("p (j o r c) -> p j o r c", o=16, r=8, c=16)
+            uv = d["u"][:].rearrange("p (j r o c) -> p j o r c", r=8, o=16, c=16)
+            sv = d["sg"][:].rearrange("p (j o c) -> p j o c", o=n, c=16)
+            nc.gpsimd.tensor_tensor(
+                out=pv[:, j, 16 - n:], in0=uv[:, j, 16 - n:],
+                in1=sv[:, j].unsqueeze(2).to_broadcast([P, n, 8, 16]), op=ALU.mult,
+            )
+
         turns = [0]
 
-        def turn(dst, src, first, last):
+        def turn(dst, src, first, last, plain=False):
             turns[0] = turns[0] + 1
-            plain = PLAIN > 0 and turns[0] % PLAIN == 0
             nc.tensor.matmul(out=dst, lhsT=src, rhs=ident[:], is_transpose=not plain, start=first, stop=last)
 
         def acc_transposes(dst, srcs):
@@ -217,31 +309,33 @@ def tile_capsulelayer_t_kernel(tc, x, W, bias, out):
 
         def s_mult(q, j):
             d = st[q]
-            if j == 0:
-                d["p"] = big.tile([P, 4096], F32, tag="big", name="p_s", align_bytes=64)
-            pv = d["p"][:].rearrange("p (a o c) -> p a o c", a=16, c=16)
-            uv = d["u"][:].rearrange("p (a o c) -> p a o c", a=16, c=16)
-            cv = d["td"][:].rearrange("p (a c) -> p a c", c=16)
-            w = 16 // S_CUT
-            for o in range(0, 16, w):
+            n = 8 - gr(q)
+            if j == 0 and n == 8:
+                d["p"] = big.tile([P, 2048 * d["nj"]], F32, tag="big", name="p_s", align_bytes=64)
+            pv = d["p"][:].rearrange("p (a o c) -> p a o c", o=16, c=16)
+            uv = d["u"][:].rearrange("p (a o c) -> p a o c", o=16, c=16)
+            cv = (d["cp"] if gr(q) > 0 and C_PS else d["td"])[:].rearrange("p (a c) -> p a c", c=16)
+            w = n // S_CUT
+            for r in range(0, n, w):
+                e = min(n, r + w)
                 nc.vector.tensor_tensor(
-                    out=pv[:, 8 * j:8 * j + 8, o:o + w], in0=uv[:, 8 * j:8 * j + 8, o:o + w],
-                    in1=cv[:, 8 * j:8 * j + 8, :].unsqueeze(2).to_broadcast([P, 8, w, 16]), op=ALU.mult,
+                    out=pv[:, 8 * j + r:8 * j + e], in0=uv[:, 8 * j + r:8 * j + e],
+                    in1=cv[:, 8 * j + r:8 * j + e, :].unsqueeze(2).to_broadcast([P, e - r, 16, 16]), op=ALU.mult,
                 )
 
         def s_acc(q, k, j):
             d = st[q]
             src = d["u"] if k == 0 else d["p"]
-            sv = src[:].rearrange("p (j r h k) -> p j r h k", j=2, r=8, h=2)
+            sv = src[:].rearrange("p (j r h k) -> p j r h k", r=8, h=2, k=P)
             if j == 0:
-                d["acc"] = ps_sh.tile([P, 2, 2, P], F32, tag="sh", name="acc_s")
+                d["acc"] = ps_sh.tile([P, d["nj"], 2, P], F32, tag="sh", name="acc_s")
             for h in range(2):
-                acc_transposes(d["acc"][:, j, h, :], [sv[:, j, r, h, :] for r in range(8)])
+                acc_transposes(d["acc"][:, j, h, :], [sv[:, j, r, h, :] for r in range(8 - (HS if k > 0 and q >= G_FROM else 0))])
 
         def s_evac(q, k):
             d = st[q]
-            d["ta"] = un.tile([P, 512], F32, tag="ta", name="ta")
-            tv = d["ta"][:].rearrange("p (j h b) -> p j h b", j=2, h=2)
+            d["ta"] = un.tile([P, 256 * d["nj"]], F32, tag="ta", name="ta")
+            tv = d["ta"][:].rearrange("p (j h b) -> p j h b", h=2, b=P)
             for h in range(2):
                 nc.scalar.activation(
                     out=tv[:, :, h, :], in_=d["acc"][:, :, h, :], func=ACT.Identity,
@@ -250,106 +344,112 @@ def tile_capsulelayer_t_kernel(tc, x, W, bias, out):
 
         def s_back(q):
             d = st[q]
-            d["s"] = ps_lg.tile([P, 512], F32, tag="lg", name="back_s")
-            for jh in range(4):
-                turn(d["s"][:, jh * P:(jh + 1) * P], d["ta"][:, jh * P:(jh + 1) * P], True, True)
+            d["s"] = ps_lg.tile([P, 256 * d["nj"]], F32, tag="lg", name="back_s")
+            for jh in range(2 * d["nj"]):
+                turn(d["s"][:, jh * P:(jh + 1) * P], d["ta"][:, jh * P:(jh + 1) * P], True, True, SB_PLAIN)
 
         def n2_pe(q, k):
-            return N2_PE and (k > 0 or q not in S0_V)
+            return N2_PE and (k > 0 or not (q in S0_V or q in MXS0))
 
         def sq_square(q, k):
             d = st[q]
-            d["sq"] = un.tile([P, 512], F32, tag="sq", name="sq")
+            d["sq"] = un.tile([P, 256 * d["nj"]], F32, tag="sq", name="sq")
             src = d["ta"] if n2_pe(q, k) else d["s"]
-            nc.scalar.activation(out=d["sq"][:], in_=src[:], func=ACT.Square)
+            if G_SQ and k < 2 and q >= G_FROM and n2_pe(q, k):
+                nc.gpsimd.tensor_tensor(out=d["sq"][:], in0=src[:], in1=src[:], op=ALU.mult)
+            else:
+                nc.scalar.activation(out=d["sq"][:], in_=src[:], func=ACT.Square)
 
         def sq_n2(q, k):
             d = st[q]
             if n2_pe(q, k):
-                d["n2"] = ps_sh.tile([P, 32], F32, tag="sh", name="n2p")
-                for jh in range(4):
+                d["n2"] = ps_sh.tile([P, 16 * d["nj"]], F32, tag="sh", name="n2p")
+                for jh in range(2 * d["nj"]):
                     nc.tensor.matmul(
                         out=d["n2"][:, (jh // 2) * 16:(jh // 2) * 16 + 16], lhsT=d["sq"][:, jh * P:(jh + 1) * P],
                         rhs=sel[:], start=(jh % 2 == 0), stop=(jh % 2 == 1),
                     )
             else:
-                d["n2"] = un.tile([P, 32], F32, tag="n2", name="n2")
+                d["n2"] = un.tile([P, 16 * d["nj"]], F32, tag="n2", name="n2")
                 nc.vector.tensor_reduce(
-                    out=d["n2"][:].rearrange("p (j c) -> p j c", j=2),
-                    in_=d["sq"][:].rearrange("p (j o c) -> p j c o", j=2, c=16),
+                    out=d["n2"][:].rearrange("p (j c) -> p j c", c=16),
+                    in_=d["sq"][:].rearrange("p (j o c) -> p j c o", o=16, c=16),
                     axis=AX.X, op=ALU.add,
                 )
 
         def sq_rd(q):
             d = st[q]
-            d["rd"] = un.tile([P, 32], F32, tag="rd", name="rd")
+            d["rd"] = un.tile([P, 16 * d["nj"]], F32, tag="rd", name="rd")
             if RD_S:
                 nc.scalar.activation(out=d["rd"][:], in_=d["n2"][:], func=ACT.Identity, bias=1.0 + EPS)
             else:
                 nc.vector.tensor_scalar(out=d["rd"][:], in0=d["n2"][:], scalar1=1.0 + EPS, scalar2=None, op0=ALU.add)
-            d["nn"] = un.tile([P, 32], F32, tag="nn", name="nn")
+            d["nn"] = un.tile([P, 16 * d["nj"]], F32, tag="nn", name="nn")
             nc.scalar.activation(out=d["nn"][:], in_=d["n2"][:], func=ACT.Sqrt, bias=tinyb[:, 0:1])
 
         def sq_gain(q):
             d = st[q]
             nc.vector.reciprocal(out=d["rd"][:], in_=d["rd"][:])
-            d["gain"] = un.tile([P, 32], F32, tag="gain", name="gain")
+            d["gain"] = un.tile([P, 16 * d["nj"]], F32, tag="gain", name="gain")
             nc.vector.tensor_mul(out=d["gain"][:], in0=d["nn"][:], in1=d["rd"][:])
 
-        def a_mult(q, j):
+        def a_mult(q, k, j):
             d = st[q]
-            if j == 0:
-                d["pa"] = big.tile([P, 4096], F32, tag="big", name="p_a", align_bytes=64)
-            pv = d["pa"][:].rearrange("p (j o r c) -> p j o r c", j=2, o=16, c=16)
-            uv = d["u"][:].rearrange("p (j r o c) -> p j o r c", j=2, r=8, c=16)
-            sv = d["s"][:].rearrange("p (j o c) -> p j o c", j=2, c=16)
-            w = 16 // A_CUT
-            for o in range(0, 16, w):
+            n = 16 - go(q, k)
+            if j == 0 and n == 16:
+                d["pa"] = big.tile([P, 2048 * d["nj"]], F32, tag="big", name="p_a", align_bytes=64)
+            pv = d["pa"][:].rearrange("p (j o r c) -> p j o r c", o=16, r=8, c=16)
+            uv = d["u"][:].rearrange("p (j r o c) -> p j o r c", r=8, o=16, c=16)
+            sv = d["s"][:].rearrange("p (j o c) -> p j o c", o=16, c=16)
+            w = n // A_CUT
+            for o in range(0, n, w):
+                e = min(n, o + w)
                 nc.vector.tensor_tensor(
-                    out=pv[:, j, o:o + w], in0=uv[:, j, o:o + w],
-                    in1=sv[:, j, o:o + w].unsqueeze(2).to_broadcast([P, w, 8, 16]), op=ALU.mult,
+                    out=pv[:, j, o:e], in0=uv[:, j, o:e],
+                    in1=sv[:, j, o:e].unsqueeze(2).to_broadcast([P, e - o, 8, 16]), op=ALU.mult,
                 )
 
         def a_acc(q, j):
             d = st[q]
-            pk = d["pa"][:].rearrange("p (j o k) -> p j o k", j=2, o=16)
+            pk = d["pa"][:].rearrange("p (j o k) -> p j o k", o=16, k=P)
             if j == 0:
-                d["acca"] = ps_sh.tile([P, 2, P], F32, tag="sh", name="acc_a")
-            acc_transposes(d["acca"][:, j, :], [pk[:, j, o, :] for o in range(16)])
+                d["acca"] = ps_sh.tile([P, d["nj"], P], F32, tag="sh", name="acc_a")
+            acc_transposes(d["acca"][:, j, :], [pk[:, j, o, :] for o in range(16 - (HA if q >= G_FROM else 0))])
 
         def a_evac(q):
             d = st[q]
-            d["tb"] = un.tile([P, 256], F32, tag="tb", name="tb")
-            nc.scalar.copy(out=d["tb"][:].rearrange("p (j b) -> p j b", j=2), in_=d["acca"][:])
+            d["tb"] = un.tile([P, P * d["nj"]], F32, tag="tb", name="tb")
+            nc.scalar.copy(out=d["tb"][:].rearrange("p (j b) -> p j b", b=P), in_=d["acca"][:])
 
         def a_back(q):
             d = st[q]
-            d["araw"] = ps_sh.tile([P, 256], F32, tag="sh", name="back_a")
-            for j in range(2):
-                turn(d["araw"][:, j * P:(j + 1) * P], d["tb"][:, j * P:(j + 1) * P], True, True)
+            d["araw"] = ps_sh.tile([P, P * d["nj"]], F32, tag="sh", name="back_a")
+            for j in range(d["nj"]):
+                turn(d["araw"][:, j * P:(j + 1) * P], d["tb"][:, j * P:(j + 1) * P], True, True, AB_PLAIN)
 
         def a_logit(q, k):
             d = st[q]
-            gv = d["gain"][:].rearrange("p (j c) -> p j c", j=2).unsqueeze(2).to_broadcast([P, 2, 8, 16])
-            av = d["araw"][:].rearrange("p (j r c) -> p j r c", j=2, c=16)
+            gv = d["gain"][:].rearrange("p (j c) -> p j c", c=16).unsqueeze(2).to_broadcast([P, d["nj"], 8, 16])
+            av = d["araw"][:].rearrange("p (j r c) -> p j r c", r=8, c=16)
             if k == 0:
-                d["logit"] = un.tile([P, 256], F32, tag="logit", name="logit")
+                d["logit"] = u_pool.tile([P, P * d["nj"]], F32, tag="logit%d" % q, name="logit")
                 nc.vector.tensor_tensor(
-                    out=d["logit"][:].rearrange("p (j r c) -> p j r c", j=2, c=16), in0=av, in1=gv, op=ALU.mult
+                    out=d["logit"][:].rearrange("p (j r c) -> p j r c", r=8, c=16), in0=av, in1=gv, op=ALU.mult
                 )
             else:
                 tmp = d["tb"]
                 nc.vector.tensor_tensor(
-                    out=tmp[:].rearrange("p (j r c) -> p j r c", j=2, c=16), in0=av, in1=gv, op=ALU.mult
+                    out=tmp[:].rearrange("p (j r c) -> p j r c", r=8, c=16), in0=av, in1=gv, op=ALU.mult
                 )
-                nc.vector.tensor_add(out=d["logit"][:], in0=tmp[:], in1=d["logit"][:])
+                eng = nc.gpsimd if G_ADD and q >= G_FROM else nc.vector
+                eng.tensor_tensor(out=d["logit"][:], in0=tmp[:], in1=d["logit"][:], op=ALU.add)
             lv = d["logit"][:].rearrange("p (a c) -> p a c", c=16)
-            d["mx"] = un.tile([P, 16], F32, tag="mx", name="mx")
+            d["mx"] = un.tile([P, 8 * d["nj"]], F32, tag="mx", name="mx")
             nc.vector.tensor_reduce(out=d["mx"][:], in_=lv, axis=AX.X, op=ALU.max)
-            d["td"] = un.tile([P, 256], F32, tag="td", name="td")
-            nc.vector.tensor_tensor(
+            d["td"] = un.tile([P, P * d["nj"]], F32, tag="td", name="td")
+            (nc.gpsimd if G_SUB and q >= G_FROM else nc.vector).tensor_tensor(
                 out=d["td"][:].rearrange("p (a c) -> p a c", c=16), in0=lv,
-                in1=d["mx"][:].unsqueeze(2).to_broadcast([P, 16, 16]), op=ALU.subtract,
+                in1=d["mx"][:].unsqueeze(2).to_broadcast([P, 8 * d["nj"], 16]), op=ALU.subtract,
             )
 
         def a_exp(q):
@@ -361,61 +461,57 @@ def tile_capsulelayer_t_kernel(tc, x, W, bias, out):
             ev = d["td"][:].rearrange("p (a c) -> p a c", c=16)
             nc.vector.tensor_reduce(out=d["mx"][:], in_=ev, axis=AX.X, op=ALU.add)
             nc.vector.reciprocal(out=d["mx"][:], in_=d["mx"][:])
-            nc.vector.tensor_tensor(
-                out=ev, in0=ev, in1=d["mx"][:].unsqueeze(2).to_broadcast([P, 16, 16]), op=ALU.mult
+            (nc.gpsimd if G_NORM and q >= G_FROM else nc.vector).tensor_tensor(
+                out=ev, in0=ev, in1=d["mx"][:].unsqueeze(2).to_broadcast([P, 8 * d["nj"], 16]), op=ALU.mult
             )
 
         def out_v(q):
             d = st[q]
             nc.vector.tensor_tensor(
-                out=d["ta"][:].rearrange("p (j c o) -> p j c o", j=2, o=16),
-                in0=d["s"][:].rearrange("p (j o c) -> p j c o", j=2, c=16),
-                in1=d["gain"][:].rearrange("p (j c) -> p j c", j=2).unsqueeze(3).to_broadcast([P, 2, 16, 16]),
+                out=d["ta"][:].rearrange("p (j c o) -> p j c o", c=16, o=16),
+                in0=d["s"][:].rearrange("p (j o c) -> p j c o", o=16, c=16),
+                in1=d["gain"][:].rearrange("p (j c) -> p j c", c=16).unsqueeze(3).to_broadcast([P, d["nj"], 16, 16]),
                 op=ALU.mult,
             )
             nc.sync.dma_start(
-                out=out[q * 256:(q + 1) * 256].rearrange("(j b) c o -> b j (c o)", j=2),
-                in_=d["ta"][:].rearrange("p (j k) -> p j k", j=2),
+                out=out[UNITS[q][0] * P:(UNITS[q][-1] + 1) * P].rearrange("(j b) c o -> b j (c o)", b=P),
+                in_=d["ta"][:].rearrange("p (j k) -> p j k", k=256),
             )
 
         def routing_steps(q):
             steps = []
+            js = range(st[q]["nj"])
+
+            def add(*fs):
+                for f in fs:
+                    steps.append(f)
+
             for k in range(3):
-                def add(*fs):
-                    for f in fs:
-                        steps.append(f)
-
-                def both(f, g):
-                    return lambda: (f(), g())
-
+                if k == 0 and q in MXS0:
+                    add(lambda: s0_bias(q))
                 if k > 0:
-                    if FUSE_SM:
-                        add(both(lambda: s_mult(q, 0), lambda: s_mult(q, 1)))
-                    else:
-                        add(lambda: s_mult(q, 0), lambda: s_mult(q, 1))
-                if k > 0 or q not in S0_V:
-                    if FUSE_ACC:
-                        add(both(lambda k=k: s_acc(q, k, 0), lambda k=k: s_acc(q, k, 1)))
-                    else:
-                        add(lambda k=k: s_acc(q, k, 0), lambda k=k: s_acc(q, k, 1))
-                    if FUSE_EB:
-                        add(both(lambda k=k: s_evac(q, k), lambda: s_back(q)))
-                    else:
-                        add(lambda k=k: s_evac(q, k), lambda: s_back(q))
+                    if gr(q) > 0:
+                        add(*[lambda j=j: s_mult_g(q, j) for j in js])
+                        if C_PS:
+                            add(lambda: c_copy(q))
+                    add(*[lambda j=j: s_mult(q, j) for j in js])
+                    if HS > 0 and q >= G_FROM:
+                        add(*[lambda j=j: s_half(q, j) for j in js])
+                if k > 0 or not (q in S0_V or q in MXS0):
+                    add(*[lambda j=j, k=k: s_acc(q, k, j) for j in js])
+                    add(lambda k=k: s_evac(q, k), lambda: s_back(q))
                 add(lambda k=k: sq_square(q, k))
                 if k < 2:
-                    if FUSE_SM:
-                        add(both(lambda: a_mult(q, 0), lambda: a_mult(q, 1)), lambda k=k: sq_n2(q, k))
-                    else:
-                        add(lambda: a_mult(q, 0), lambda k=k: sq_n2(q, k), lambda: a_mult(q, 1))
-                    if FUSE_ACC:
-                        add(both(lambda: a_acc(q, 0), lambda: a_acc(q, 1)), lambda: sq_rd(q), lambda: sq_gain(q))
-                    else:
-                        add(lambda: a_acc(q, 0), lambda: sq_rd(q), lambda: a_acc(q, 1), lambda: sq_gain(q))
-                    if FUSE_EB:
-                        add(both(lambda: a_evac(q), lambda: a_back(q)))
-                    else:
-                        add(lambda: a_evac(q), lambda: a_back(q))
+                    if go(q, k) > 0:
+                        add(lambda: s_copy(q))
+                        add(*[lambda j=j: a_mult_g(q, j) for j in js])
+                    add(lambda k=k: a_mult(q, k, 0), lambda k=k: sq_n2(q, k))
+                    add(*[lambda j=j, k=k: a_mult(q, k, j) for j in js if j > 0])
+                    if HA > 0 and q >= G_FROM:
+                        add(*[lambda j=j: a_half(q, j) for j in js])
+                    add(lambda: a_acc(q, 0), lambda: sq_rd(q))
+                    add(*[lambda j=j: a_acc(q, j) for j in js if j > 0])
+                    add(lambda: sq_gain(q), lambda: a_evac(q), lambda: a_back(q))
                     add(lambda k=k: a_logit(q, k), lambda: a_exp(q), lambda: a_soft(q))
                 else:
                     add(lambda k=k: sq_n2(q, k), lambda: sq_rd(q), lambda: sq_gain(q), lambda: out_v(q))
@@ -467,10 +563,10 @@ def tile_capsulelayer_t_kernel(tc, x, W, bias, out):
                         fe_quant(i - 1)
                 if o == "M" and i >= MX_LAG:
                     fe_mx(i - MX_LAG)
-                    if (i - MX_LAG) % 8 == 7:
-                        chains.append([routing_steps((i - MX_LAG) // 8), 0])
-                        if len(chains) == 1:
-                            advance(START)
+                    t = (i - MX_LAG) // 4
+                    q = unit_of[t][0]
+                    if (i - MX_LAG) % 4 == 3 and t == UNITS[q][-1]:
+                        chains.append([routing_steps(q), 0])
                 if o == "A":
                     pace(i)
         for rep in range(TAIL):

@@ -19,28 +19,28 @@ UNITS = ((0,1,),(2,3,),(4,5,),(6,7,),)
 EPS = 1e-8
 
 MANUAL = True
-EARLY_V = 0
+EARLY_V = 4
 S_CUT = 1
 A_CUT = 1
-OLD_FIRST = True
-ORDER = 'AMTQ'
+OLD_FIRST = False
+ORDER = 'MTQA'
 LATE_RATE = 1.0
 QUANT2 = True
 PLAIN = 0
-RD_S = True
-S0_V = (0,1,)
+RD_S = False
+S0_V = (0,1,2,3,)
 N2_PE = True
 X_EVAC = 'SS'
 W_EVAC = 'SS'
-RATE = 0.75
-SH_BUFS = 5
+RATE = 0.7
+SH_BUFS = 8
 LG_BUFS = 3
 BIG_BUFS = 6
-MX_LAG = 6
-TAIL = 60
+MX_LAG = 5
+TAIL = 160
 MXS0 = ()
-G_R = 3
-G_O = 4
+G_R = 2
+G_O = 5
 C_PS = True
 G_SUB = True
 G_NORM = True
@@ -48,6 +48,20 @@ G_ADD = False
 G_SQ = False
 G_FROM = 0
 S0_BUFS = 1
+MX_GRP = 1
+WE = 0.5
+HU = ()
+NN_FIRST = True
+FINE_W = True
+SPLIT_END = ()
+WN = {}
+BOOST = 0.1
+FBOOST = 0.0
+XQ_BUFS = 3
+WM = 1.5
+WG = 0.5
+WA = 1.0
+WS = 1.0
 SB_PLAIN = False
 AB_PLAIN = False
 HA = 0
@@ -60,11 +74,10 @@ def tile_capsulelayer_t_kernel(tc, x, W, bias, out):
     with ExitStack() as ctx:
         const = ctx.enter_context(tc.tile_pool(name="const", bufs=1))
         big = ctx.enter_context(tc.tile_pool(name="big", bufs=BIG_BUFS))
-        xq_pool = ctx.enter_context(tc.tile_pool(name="xq", bufs=3))
+        xq_pool = ctx.enter_context(tc.tile_pool(name="xq", bufs=XQ_BUFS))
         u_pool = ctx.enter_context(tc.tile_pool(name="u", bufs=1))
         un = ctx.enter_context(tc.tile_pool(name="un", bufs=4))
         ps_sh = ctx.enter_context(tc.psum_pool(name="pssh", bufs=SH_BUFS))
-        ps_lg = ctx.enter_context(tc.psum_pool(name="pslg", bufs=LG_BUFS))
         ps_s0 = ctx.enter_context(tc.psum_pool(name="pss0", bufs=S0_BUFS)) if len(MXS0) > 0 else None
 
         def copy_on(letter, dst, src):
@@ -98,10 +111,11 @@ def tile_capsulelayer_t_kernel(tc, x, W, bias, out):
                 fe["w%d" % (wq // 2)] = big.tile([P, 8192], BF16, tag="big", name="win", align_bytes=64)
             win = fe["w%d" % (wq // 2)]
             h = wq % 2
-            for s in range(2):
+            n = 1 if FINE_W and wq == 0 else 2
+            for s in range(0, 4, n):
                 nc.sync.dma_start(
-                    out=win[:, h * 4096 + s * 2048:h * 4096 + (s + 1) * 2048].rearrange("p (t i) -> p t i", t=2),
-                    in_=w_rows[wq * 512 + s * 256:wq * 512 + (s + 1) * 256, :].rearrange("(t p) i -> p t i", p=P),
+                    out=win[:, h * 4096 + s * 1024:h * 4096 + (s + n) * 1024].rearrange("p (t i) -> p t i", t=n),
+                    in_=w_rows[wq * 512 + s * P:wq * 512 + (s + n) * P, :].rearrange("(t p) i -> p t i", p=P),
                 )
 
         def load_bias():
@@ -195,7 +209,7 @@ def tile_capsulelayer_t_kernel(tc, x, W, bias, out):
                 if q in MXS0:
                     st[q]["s0"] = ps_s0.tile([P, 256 * st[q]["nj"]], F32, tag="s0", name="s0")
                 if q in S0_V or q in MXS0:
-                    st[q]["s"] = un.tile([P, 256 * st[q]["nj"]], F32, tag="s1", name="s1")
+                    st[q]["s"] = un.tile([P, 256 * st[q]["nj"]], F32, tag="s1", name="s1", bufs=2)
             xc = fe["xc%d" % (i // 2)]
             xs = fe["xs%d" % (i // 2)]
             rb = 4 * (jr % 2)
@@ -250,7 +264,7 @@ def tile_capsulelayer_t_kernel(tc, x, W, bias, out):
 
         def c_copy(q):
             d = st[q]
-            d["cp"] = ps_lg.tile([P, P * d["nj"]], F32, tag="lg", name="cp")
+            d["cp"] = ps_sh.tile([P, P * d["nj"]], F32, tag="sh", name="cp")
             nc.tensor.matmul(out=d["cp"][:], lhsT=ident[:], rhs=d["td"][:], start=True, stop=True)
 
         def s_mult_g(q, j):
@@ -330,7 +344,7 @@ def tile_capsulelayer_t_kernel(tc, x, W, bias, out):
             if j == 0:
                 d["acc"] = ps_sh.tile([P, d["nj"], 2, P], F32, tag="sh", name="acc_s")
             for h in range(2):
-                acc_transposes(d["acc"][:, j, h, :], [sv[:, j, r, h, :] for r in range(8 - (HS if k > 0 and q >= G_FROM else 0))])
+                acc_transposes(d["acc"][:, j, h, :], [sv[:, j, r, h, :] for r in range(8 - (HS if k > 0 and q in HU else 0))])
 
         def s_evac(q, k):
             d = st[q]
@@ -344,7 +358,7 @@ def tile_capsulelayer_t_kernel(tc, x, W, bias, out):
 
         def s_back(q):
             d = st[q]
-            d["s"] = ps_lg.tile([P, 256 * d["nj"]], F32, tag="lg", name="back_s")
+            d["s"] = ps_sh.tile([P, 256 * d["nj"]], F32, tag="sh", name="back_s")
             for jh in range(2 * d["nj"]):
                 turn(d["s"][:, jh * P:(jh + 1) * P], d["ta"][:, jh * P:(jh + 1) * P], True, True, SB_PLAIN)
 
@@ -353,7 +367,7 @@ def tile_capsulelayer_t_kernel(tc, x, W, bias, out):
 
         def sq_square(q, k):
             d = st[q]
-            d["sq"] = un.tile([P, 256 * d["nj"]], F32, tag="sq", name="sq")
+            d["sq"] = un.tile([P, 256 * d["nj"]], F32, tag="sq", name="sq", bufs=3)
             src = d["ta"] if n2_pe(q, k) else d["s"]
             if G_SQ and k < 2 and q >= G_FROM and n2_pe(q, k):
                 nc.gpsimd.tensor_tensor(out=d["sq"][:], in0=src[:], in1=src[:], op=ALU.mult)
@@ -380,12 +394,15 @@ def tile_capsulelayer_t_kernel(tc, x, W, bias, out):
         def sq_rd(q):
             d = st[q]
             d["rd"] = un.tile([P, 16 * d["nj"]], F32, tag="rd", name="rd")
+            d["nn"] = un.tile([P, 16 * d["nj"]], F32, tag="nn", name="nn")
+            if NN_FIRST:
+                nc.scalar.activation(out=d["nn"][:], in_=d["n2"][:], func=ACT.Sqrt, bias=tinyb[:, 0:1])
             if RD_S:
                 nc.scalar.activation(out=d["rd"][:], in_=d["n2"][:], func=ACT.Identity, bias=1.0 + EPS)
             else:
                 nc.vector.tensor_scalar(out=d["rd"][:], in0=d["n2"][:], scalar1=1.0 + EPS, scalar2=None, op0=ALU.add)
-            d["nn"] = un.tile([P, 16 * d["nj"]], F32, tag="nn", name="nn")
-            nc.scalar.activation(out=d["nn"][:], in_=d["n2"][:], func=ACT.Sqrt, bias=tinyb[:, 0:1])
+            if not NN_FIRST:
+                nc.scalar.activation(out=d["nn"][:], in_=d["n2"][:], func=ACT.Sqrt, bias=tinyb[:, 0:1])
 
         def sq_gain(q):
             d = st[q]
@@ -414,7 +431,7 @@ def tile_capsulelayer_t_kernel(tc, x, W, bias, out):
             pk = d["pa"][:].rearrange("p (j o k) -> p j o k", o=16, k=P)
             if j == 0:
                 d["acca"] = ps_sh.tile([P, d["nj"], P], F32, tag="sh", name="acc_a")
-            acc_transposes(d["acca"][:, j, :], [pk[:, j, o, :] for o in range(16 - (HA if q >= G_FROM else 0))])
+            acc_transposes(d["acca"][:, j, :], [pk[:, j, o, :] for o in range(16 - (HA if q in HU else 0))])
 
         def a_evac(q):
             d = st[q]
@@ -478,52 +495,132 @@ def tile_capsulelayer_t_kernel(tc, x, W, bias, out):
                 in_=d["ta"][:].rearrange("p (j k) -> p j k", k=256),
             )
 
+        def end_evac(q, j):
+            d = st[q]
+            if j == 0:
+                d["ta"] = un.tile([P, 256 * d["nj"]], F32, tag="ta", name="ta")
+            tv = d["ta"][:].rearrange("p (j h b) -> p j h b", h=2, b=P)
+            for h in range(2):
+                nc.scalar.activation(
+                    out=tv[:, j, h, :], in_=d["acc"][:, j, h, :], func=ACT.Identity, bias=bias_t[:, h:h + 1], scale=1.0
+                )
+
+        def end_back(q, j):
+            d = st[q]
+            if j == 0:
+                d["s"] = ps_sh.tile([P, 256 * d["nj"]], F32, tag="sh", name="back_s")
+                d["s1"] = ps_sh.tile([P, 256 * d["nj"]], F32, tag="sh", name="back_s1")
+            dst = d["s"] if j == 0 else d["s1"]
+            for h in range(2):
+                turn(dst[:, h * P:(h + 1) * P], d["ta"][:, (2 * j + h) * P:(2 * j + h + 1) * P], True, True)
+
+        def end_square(q, j):
+            d = st[q]
+            if j == 0:
+                d["sq"] = un.tile([P, 256 * d["nj"]], F32, tag="sq", name="sq", bufs=3)
+            nc.scalar.activation(out=d["sq"][:, j * 256:(j + 1) * 256], in_=d["ta"][:, j * 256:(j + 1) * 256], func=ACT.Square)
+
+        def end_gain(q, j):
+            d = st[q]
+            n2 = ps_sh.tile([P, 16], F32, tag="sh", name="n2e")
+            for h in range(2):
+                nc.tensor.matmul(
+                    out=n2[:], lhsT=d["sq"][:, (2 * j + h) * P:(2 * j + h + 1) * P], rhs=sel[:],
+                    start=(h == 0), stop=(h == 1),
+                )
+            nn = un.tile([P, 32], F32, tag="nn", name="nne")
+            rd = un.tile([P, 32], F32, tag="rd", name="rde")
+            gain = un.tile([P, 32], F32, tag="gain", name="gaine")
+            nc.scalar.activation(out=nn[:, 0:16], in_=n2[:], func=ACT.Sqrt, bias=tinyb[:, 0:1])
+            nc.vector.tensor_scalar(out=rd[:, 0:16], in0=n2[:], scalar1=1.0 + EPS, scalar2=None, op0=ALU.add)
+            nc.vector.reciprocal(out=rd[:, 0:16], in_=rd[:, 0:16])
+            nc.vector.tensor_mul(out=gain[:, 0:16], in0=nn[:, 0:16], in1=rd[:, 0:16])
+            d["g%d" % j] = gain
+
+        def end_out(q, j):
+            d = st[q]
+            src = d["s"] if j == 0 else d["s1"]
+            nc.vector.tensor_tensor(
+                out=d["ta"][:, j * 256:(j + 1) * 256].rearrange("p (c o) -> p c o", o=16),
+                in0=src[:, 0:256].rearrange("p (o c) -> p c o", c=16),
+                in1=d["g%d" % j][:, 0:16].unsqueeze(2).to_broadcast([P, 16, 16]), op=ALU.mult,
+            )
+            nc.sync.dma_start(
+                out=out[UNITS[q][j] * P:(UNITS[q][j] + 1) * P].rearrange("b c o -> b (c o)"),
+                in_=d["ta"][:, j * 256:(j + 1) * 256],
+            )
+
         def routing_steps(q):
             steps = []
             js = range(st[q]["nj"])
 
-            def add(*fs):
+            def add(*fs, w=None, n="x"):
                 for f in fs:
-                    steps.append(f)
+                    steps.append((f, WN.get(n, WS if w is None else w)))
 
             for k in range(3):
                 if k == 0 and q in MXS0:
-                    add(lambda: s0_bias(q))
+                    add(lambda: s0_bias(q), n="s0b")
                 if k > 0:
                     if gr(q) > 0:
-                        add(*[lambda j=j: s_mult_g(q, j) for j in js])
+                        add(*[lambda j=j: s_mult_g(q, j) for j in js], w=WG, n="smg")
                         if C_PS:
-                            add(lambda: c_copy(q))
-                    add(*[lambda j=j: s_mult(q, j) for j in js])
-                    if HS > 0 and q >= G_FROM:
-                        add(*[lambda j=j: s_half(q, j) for j in js])
+                            add(lambda: c_copy(q), n="cc")
+                    add(*[lambda j=j: s_mult(q, j) for j in js], w=WM, n="sm")
+                    if HS > 0 and q in HU:
+                        add(*[lambda j=j: s_half(q, j) for j in js], w=WG, n="sh")
+                if k == 2 and q in SPLIT_END:
+                    ends = [
+                        lambda j: s_acc(q, 2, j),
+                        lambda j: end_evac(q, j),
+                        lambda j: (end_square(q, j), end_back(q, j)),
+                        lambda j: end_gain(q, j),
+                        lambda j: end_out(q, j),
+                    ]
+                    for i in range(5 + 2 * (len(js) - 1)):
+                        for j in js:
+                            if 0 <= i - 2 * j < 5:
+                                add(lambda f=ends[i - 2 * j], j=j: f(j), w=WE)
+                    continue
                 if k > 0 or not (q in S0_V or q in MXS0):
-                    add(*[lambda j=j, k=k: s_acc(q, k, j) for j in js])
-                    add(lambda k=k: s_evac(q, k), lambda: s_back(q))
-                add(lambda k=k: sq_square(q, k))
+                    add(*[lambda j=j, k=k: s_acc(q, k, j) for j in js], w=WA, n="sa")
+                    add(lambda k=k: s_evac(q, k), n="se")
+                    add(lambda: s_back(q), n="sb")
+                add(lambda k=k: sq_square(q, k), n="sq")
                 if k < 2:
                     if go(q, k) > 0:
-                        add(lambda: s_copy(q))
-                        add(*[lambda j=j: a_mult_g(q, j) for j in js])
-                    add(lambda k=k: a_mult(q, k, 0), lambda k=k: sq_n2(q, k))
-                    add(*[lambda j=j, k=k: a_mult(q, k, j) for j in js if j > 0])
-                    if HA > 0 and q >= G_FROM:
-                        add(*[lambda j=j: a_half(q, j) for j in js])
-                    add(lambda: a_acc(q, 0), lambda: sq_rd(q))
-                    add(*[lambda j=j: a_acc(q, j) for j in js if j > 0])
-                    add(lambda: sq_gain(q), lambda: a_evac(q), lambda: a_back(q))
-                    add(lambda k=k: a_logit(q, k), lambda: a_exp(q), lambda: a_soft(q))
+                        add(lambda: s_copy(q), n="sc")
+                        add(*[lambda j=j: a_mult_g(q, j) for j in js], w=WG, n="amg")
+                    add(lambda k=k: a_mult(q, k, 0), w=WM, n="am")
+                    add(lambda k=k: sq_n2(q, k), n="n2")
+                    add(*[lambda j=j, k=k: a_mult(q, k, j) for j in js if j > 0], w=WM, n="am")
+                    if HA > 0 and q in HU:
+                        add(*[lambda j=j: a_half(q, j) for j in js], w=WG, n="ah")
+                    add(lambda: a_acc(q, 0), w=WA, n="aa")
+                    add(lambda: sq_rd(q), n="rd")
+                    add(*[lambda j=j: a_acc(q, j) for j in js if j > 0], w=WA, n="aa")
+                    add(lambda: sq_gain(q), n="ga")
+                    add(lambda: a_evac(q), n="ae")
+                    add(lambda: a_back(q), n="ab")
+                    add(lambda k=k: a_logit(q, k), n="lo")
+                    add(lambda: a_exp(q), n="ex")
+                    add(lambda: a_soft(q), n="so")
                 else:
-                    add(lambda k=k: sq_n2(q, k), lambda: sq_rd(q), lambda: sq_gain(q), lambda: out_v(q))
+                    add(lambda k=k: sq_n2(q, k), n="n2")
+                    add(lambda: sq_rd(q), n="rd")
+                    add(lambda: sq_gain(q), n="ga")
+                    add(lambda: out_v(q), n="ov")
             return steps
 
         chains = []
 
-        def advance(n):
+        def advance(n, boost=0.0):
             for rep in range(n):
                 for ch in (chains if OLD_FIRST else chains[::-1]):
-                    if ch[1] < len(ch[0]):
-                        ch[0][ch[1]]()
+                    ch[2] = ch[2] + 1.0 + boost * ch[3]
+                    while ch[1] < len(ch[0]) and ch[2] >= 0.999:
+                        ch[0][ch[1]][0]()
+                        ch[2] = ch[2] - ch[0][ch[1]][1]
                         ch[1] = ch[1] + 1
 
         load_w(0)
@@ -543,7 +640,7 @@ def tile_capsulelayer_t_kernel(tc, x, W, bias, out):
             owed[0] = owed[0] + (RATE if i < 32 else LATE_RATE)
             while owed[0] >= 1.0:
                 owed[0] = owed[0] - 1.0
-                advance(1)
+                advance(1, FBOOST)
 
         for i in range(32 + MX_LAG):
             for o in ORDER:
@@ -561,13 +658,14 @@ def tile_capsulelayer_t_kernel(tc, x, W, bias, out):
                         w_quant(i)
                     if 0 <= i - 1 < 32:
                         fe_quant(i - 1)
-                if o == "M" and i >= MX_LAG:
-                    fe_mx(i - MX_LAG)
+                if o == "M" and i >= MX_LAG and (i - MX_LAG) % MX_GRP == MX_GRP - 1:
+                    for b in range(i - MX_LAG - MX_GRP + 1, i - MX_LAG + 1):
+                        fe_mx(b)
                     t = (i - MX_LAG) // 4
                     q = unit_of[t][0]
                     if (i - MX_LAG) % 4 == 3 and t == UNITS[q][-1]:
-                        chains.append([routing_steps(q), 0])
+                        chains.append([routing_steps(q), 0, 0.0, q])
                 if o == "A":
                     pace(i)
         for rep in range(TAIL):
-            advance(1)
+            advance(1, BOOST)

@@ -19,20 +19,20 @@ UNITS = ((0,1,),(2,3,),(4,5,),(6,7,),)
 EPS = 1e-8
 
 MANUAL = True
-EARLY_V = 4
+EARLY_V = 8
 S_CUT = 1
 A_CUT = 1
 OLD_FIRST = False
-ORDER = 'MTQA'
+ORDER = 'TAMQ'
 LATE_RATE = 1.0
 QUANT2 = True
 PLAIN = 0
-RD_S = False
-S0_V = (0,1,2,3,)
+RD_S = True
+S0_V = (0,1,2,)
 N2_PE = True
 X_EVAC = 'SS'
 W_EVAC = 'SS'
-RATE = 0.7
+RATE = 0.6
 SH_BUFS = 8
 LG_BUFS = 3
 BIG_BUFS = 6
@@ -40,7 +40,7 @@ MX_LAG = 5
 TAIL = 160
 MXS0 = ()
 G_R = 2
-G_O = 5
+G_O = 0
 C_PS = True
 G_SUB = True
 G_NORM = True
@@ -49,17 +49,21 @@ G_SQ = False
 G_FROM = 0
 S0_BUFS = 1
 MX_GRP = 1
+SPL_GA = True
+SPL_LO = False
+SPL_SO = False
+WL = 0.5
 WE = 0.5
 HU = ()
 NN_FIRST = True
 FINE_W = True
-SPLIT_END = ()
+SPLIT_END = (3,)
 WN = {}
 BOOST = 0.1
 FBOOST = 0.0
 XQ_BUFS = 3
 WM = 1.5
-WG = 0.5
+WG = 0.75
 WA = 1.0
 WS = 1.0
 SB_PLAIN = False
@@ -404,9 +408,12 @@ def tile_capsulelayer_t_kernel(tc, x, W, bias, out):
             if not NN_FIRST:
                 nc.scalar.activation(out=d["nn"][:], in_=d["n2"][:], func=ACT.Sqrt, bias=tinyb[:, 0:1])
 
-        def sq_gain(q):
+        def sq_recip(q):
             d = st[q]
             nc.vector.reciprocal(out=d["rd"][:], in_=d["rd"][:])
+
+        def sq_gain(q):
+            d = st[q]
             d["gain"] = un.tile([P, 16 * d["nj"]], F32, tag="gain", name="gain")
             nc.vector.tensor_mul(out=d["gain"][:], in0=d["nn"][:], in1=d["rd"][:])
 
@@ -460,6 +467,9 @@ def tile_capsulelayer_t_kernel(tc, x, W, bias, out):
                 )
                 eng = nc.gpsimd if G_ADD and q >= G_FROM else nc.vector
                 eng.tensor_tensor(out=d["logit"][:], in0=tmp[:], in1=d["logit"][:], op=ALU.add)
+
+        def a_max(q):
+            d = st[q]
             lv = d["logit"][:].rearrange("p (a c) -> p a c", c=16)
             d["mx"] = un.tile([P, 8 * d["nj"]], F32, tag="mx", name="mx")
             nc.vector.tensor_reduce(out=d["mx"][:], in_=lv, axis=AX.X, op=ALU.max)
@@ -473,10 +483,14 @@ def tile_capsulelayer_t_kernel(tc, x, W, bias, out):
             d = st[q]
             nc.scalar.activation(out=d["td"][:], in_=d["td"][:], func=ACT.Exp)
 
-        def a_soft(q):
+        def a_sum(q):
             d = st[q]
             ev = d["td"][:].rearrange("p (a c) -> p a c", c=16)
             nc.vector.tensor_reduce(out=d["mx"][:], in_=ev, axis=AX.X, op=ALU.add)
+
+        def a_soft(q):
+            d = st[q]
+            ev = d["td"][:].rearrange("p (a c) -> p a c", c=16)
             nc.vector.reciprocal(out=d["mx"][:], in_=d["mx"][:])
             (nc.gpsimd if G_NORM and q >= G_FROM else nc.vector).tensor_tensor(
                 out=ev, in0=ev, in1=d["mx"][:].unsqueeze(2).to_broadcast([P, 8 * d["nj"], 16]), op=ALU.mult
@@ -599,16 +613,28 @@ def tile_capsulelayer_t_kernel(tc, x, W, bias, out):
                     add(lambda: a_acc(q, 0), w=WA, n="aa")
                     add(lambda: sq_rd(q), n="rd")
                     add(*[lambda j=j: a_acc(q, j) for j in js if j > 0], w=WA, n="aa")
-                    add(lambda: sq_gain(q), n="ga")
-                    add(lambda: a_evac(q), n="ae")
+                    if SPL_GA:
+                        add(lambda: sq_recip(q), n="ga")
+                        add(lambda: (a_evac(q), sq_gain(q)), n="ae")
+                    else:
+                        add(lambda: (sq_recip(q), sq_gain(q)), n="ga")
+                        add(lambda: a_evac(q), n="ae")
                     add(lambda: a_back(q), n="ab")
-                    add(lambda k=k: a_logit(q, k), n="lo")
+                    if SPL_LO:
+                        add(lambda k=k: a_logit(q, k), n="lo", w=WL)
+                        add(lambda: a_max(q), n="mx")
+                    else:
+                        add(lambda k=k: (a_logit(q, k), a_max(q)), n="lo")
                     add(lambda: a_exp(q), n="ex")
-                    add(lambda: a_soft(q), n="so")
+                    if SPL_SO:
+                        add(lambda: a_sum(q), n="so", w=WL)
+                        add(lambda: a_soft(q), n="so2")
+                    else:
+                        add(lambda: (a_sum(q), a_soft(q)), n="so")
                 else:
                     add(lambda k=k: sq_n2(q, k), n="n2")
                     add(lambda: sq_rd(q), n="rd")
-                    add(lambda: sq_gain(q), n="ga")
+                    add(lambda: (sq_recip(q), sq_gain(q)), n="ga")
                     add(lambda: out_v(q), n="ov")
             return steps
 

from contextlib import ExitStack

import concourse.mybir as mybir
from concourse.masks import make_identity

F32 = mybir.dt.float32
BF16 = mybir.dt.bfloat16
U32 = mybir.dt.uint32
U8 = mybir.dt.uint8
FP8X4 = mybir.dt.float8_e4m3fn_x4
ALU = mybir.AluOpType
ACT = mybir.ActivationFunctionType
AX = mybir.AxisListType

FLOPS = 2 * 1024 * 8 * 256 * 1024

P = 128
UNITS = ((0,1,),(2,3,),(4,5,),(6,7,),)
EPS = 1e-8

MANUAL = True
EARLY_V = 8
S_CUT = 1
A_CUT = 1
OLD_FIRST = False
ORDER = 'TAMQ'
LATE_RATE = 1.0
QUANT2 = True
PLAIN = 0
RD_S = True
S0_V = (0,1,2,)
N2_PE = True
X_EVAC = 'SS'
W_EVAC = 'SS'
RATE = 0.6
SH_BUFS = 8
LG_BUFS = 3
BIG_BUFS = 6
MX_LAG = 5
TAIL = 160
MXS0 = ()
G_R = 2
G_O = 0
C_PS = True
G_SUB = True
G_NORM = True
G_ADD = False
G_SQ = False
G_FROM = 0
S0_BUFS = 1
MX_GRP = 1
SPL_GA = True
SPL_LO = False
SPL_SO = False
WL = 0.5
WE = 0.5
HU = ()
NN_FIRST = True
FINE_W = True
SPLIT_END = (3,)
WN = {}
BOOST = 0.1
FBOOST = 0.0
XQ_BUFS = 3
WM = 1.5
WG = 0.75
WA = 1.0
WS = 1.0
SB_PLAIN = False
AB_PLAIN = False
HA = 0
HS = 0
CP_BUFS = 1


def tile_capsulelayer_t_kernel(tc, x, W, bias, out):
    nc = tc.nc
    with ExitStack() as ctx:
        const = ctx.enter_context(tc.tile_pool(name="const", bufs=1))
        big = ctx.enter_context(tc.tile_pool(name="big", bufs=BIG_BUFS))
        xq_pool = ctx.enter_context(tc.tile_pool(name="xq", bufs=XQ_BUFS))
        u_pool = ctx.enter_context(tc.tile_pool(name="u", bufs=1))
        un = ctx.enter_context(tc.tile_pool(name="un", bufs=4))
        ps_sh = ctx.enter_context(tc.psum_pool(name="pssh", bufs=SH_BUFS))
        ps_s0 = ctx.enter_context(tc.psum_pool(name="pss0", bufs=S0_BUFS)) if len(MXS0) > 0 else None

        def copy_on(letter, dst, src):
            if letter == "S":
                nc.scalar.copy(out=dst, in_=src)
            else:
                nc.vector.tensor_copy(out=dst, in_=src)

        ident = const.tile([P, P], F32, name="ident")
        make_identity(nc, ident[:])
        tinyb = const.tile([P, 1], F32, name="tinyb")
        nc.vector.memset(tinyb[:], 1e-30)
        wc = const.tile([P, 8, 512], U32, name="wc", align_bytes=64)
        ws = const.tile([P, 8, 512], U8, name="ws", align_bytes=64)
        bias_t = const.tile([P, 2], F32, name="bias_t")
        braw = const.tile([P, 256], BF16, name="braw")
        bc = const.tile([P, 256], F32, name="bc")
        sel = const.tile([P, 16], F32, name="sel")

        w_rows = W.rearrange("r c o i -> (r c o) i")
        fe = dict()
        st = [dict() for q in UNITS]
        unit_of = dict()
        for q in range(len(UNITS)):
            for j in range(len(UNITS[q])):
                unit_of[UNITS[q][j]] = (q, j)
            st[q]["nj"] = len(UNITS[q])

        def load_w(wq):
            if wq % 2 == 0:
                fe["w%d" % (wq // 2)] = big.tile([P, 8192], BF16, tag="big", name="win", align_bytes=64)
            win = fe["w%d" % (wq // 2)]
            h = wq % 2
            n = 1 if FINE_W and wq == 0 else 2
            for s in range(0, 4, n):
                nc.sync.dma_start(
                    out=win[:, h * 4096 + s * 1024:h * 4096 + (s + n) * 1024].rearrange("p (t i) -> p t i", t=n),
                    in_=w_rows[wq * 512 + s * P:wq * 512 + (s + n) * P, :].rearrange("(t p) i -> p t i", p=P),
                )

        def load_bias():
            nc.sync.dma_start(out=braw[:], in_=bias.rearrange("a b c o -> (a b c o)").partition_broadcast(P))

        def prep_bias():
            nc.vector.tensor_copy(
                out=bc[:].rearrange("p (o c) -> p o c", c=16),
                in_=braw[:].rearrange("p (c o) -> p o c", o=16),
            )
            nc.vector.tensor_reduce(
                out=sel[:], in_=ident[:].rearrange("p (o c) -> p c o", c=16), axis=AX.X, op=ALU.add
            )
            tpb = ps_sh.tile([P, 4, P], F32, tag="sh", name="tpb")
            for h in range(2):
                nc.tensor.transpose(out=tpb[:, h, :], in_=bc[:, h * P:(h + 1) * P], identity=ident[:])
            for h in range(2):
                nc.vector.tensor_copy(out=bias_t[:, h:h + 1], in_=tpb[:, h, 0:1])

        def w_step(wq):
            wt, sub = divmod(wq, 2)
            if sub == 0:
                fe["gw%d" % wt] = big.tile([P, 8192], BF16, tag="big", name="grpw", align_bytes=64)
            ww = fe["w%d" % wt][:].bitcast(F32)
            grp = fe["gw%d" % wt]
            gv = grp[:].bitcast(F32).rearrange("p (r g o c u) -> p r g o c u", r=4, g=2, o=16, c=16, u=2)
            for rl in range(2 * sub, 2 * sub + 2):
                for h in range(2):
                    t = rl * 2 + h
                    tp = ps_sh.tile([P, 4, P], F32, tag="sh", name="tpw")
                    for k in range(4):
                        at = t * 512 + (k // 2) * 256 + k % 2
                        nc.tensor.transpose(out=tp[:, k, :], in_=ww[:, at: at - k % 2 + 256: 2], identity=ident[:])
                    for g in range(2):
                        copy_on(
                            W_EVAC[h],
                            gv[:, rl, g, :, 8 * h:8 * h + 8, :],
                            tp[:, 2 * g:2 * g + 2, :].rearrange("p u (c o) -> p o c u", o=16),
                        )

        def w_quant(wq):
            sub = wq % 2
            grp = fe["gw%d" % (wq // 2)]
            nc.vector.quantize_mx(
                out=wc[:, 2 * wq:2 * wq + 2, :].rearrange("p a b -> p (a b)").bitcast(FP8X4),
                scales=ws[:, 2 * wq:2 * wq + 2, :].rearrange("p a b -> p (a b)"),
                in_=grp[:, sub * 4096:(sub + 1) * 4096],
            )

        def load_x(t, half):
            if half == 0:
                fe["x%d" % t] = big.tile([P, 8192], BF16, tag="big", name="xin", align_bytes=64)
            nc.sync.dma_start(
                out=fe["x%d" % t][:, half * 4096:(half + 1) * 4096],
                in_=x[t * P:(t + 1) * P, 4 * half:4 * half + 4, :].rearrange("b r i -> b (r i)"),
            )

        def fe_transposes(i):
            t, jr = divmod(i, 4)
            if jr == 0:
                fe["g%d" % t] = big.tile([P, 8192], BF16, tag="big", name="grpx", align_bytes=64)
            xw = fe["x%d" % t][:].bitcast(F32)
            gv = fe["g%d" % t][:].bitcast(F32).rearrange("p (r g b u) -> p r g b u", r=8, g=2, b=P, u=2)
            for rr in range(2):
                r = 2 * jr + rr
                tp = ps_sh.tile([P, 4, P], F32, tag="sh", name="tpx")
                for k in range(4):
                    at = r * 512 + (k // 2) * 256 + k % 2
                    nc.tensor.transpose(out=tp[:, k, :], in_=xw[:, at: at - k % 2 + 256: 2], identity=ident[:])
                copy_on("V" if rr == 1 and i < EARLY_V else X_EVAC[rr], gv[:, r], tp[:].rearrange("p (g u) b -> p g b u", u=2))

        def fe_quant(i):
            t, jr = divmod(i, 4)
            if jr % 2 == 0:
                return
            xc = xq_pool.tile([P, 8, P], U32, tag="xc", name="xc", align_bytes=64)
            xs = xq_pool.tile([P, 8, P], U8, tag="xs", name="xs", align_bytes=64)
            fe["xc%d" % (i // 2)] = xc
            fe["xs%d" % (i // 2)] = xs
            nc.vector.quantize_mx(
                out=xc[:].rearrange("p a b -> p (a b)").bitcast(FP8X4),
                scales=xs[:].rearrange("p a b -> p (a b)"),
                in_=fe["g%d" % t][:, (jr - 1) * 2048:(jr + 1) * 2048],
            )

        def fe_mx(i):
            t, jr = divmod(i, 4)
            q, j = unit_of[t]
            if j == 0 and jr == 0:
                st[q]["u"] = u_pool.tile([P, 2048 * st[q]["nj"]], F32, tag="u%d" % q, name="u")
                if q in MXS0:
                    st[q]["s0"] = ps_s0.tile([P, 256 * st[q]["nj"]], F32, tag="s0", name="s0")
                if q in S0_V or q in MXS0:
                    st[q]["s"] = un.tile([P, 256 * st[q]["nj"]], F32, tag="s1", name="s1", bufs=2)
            xc = fe["xc%d" % (i // 2)]
            xs = fe["xs%d" % (i // 2)]
            rb = 4 * (jr % 2)
            u = st[q]["u"]
            ups = ps_sh.tile([P, 512], F32, tag="sh", name="ups")
            for rr in range(2):
                r = 2 * jr + rr
                for g in range(2):
                    nc.tensor.matmul_mx(
                        out=ups[:, rr * 256:(rr + 1) * 256],
                        lhsT=xc[:, rb + 2 * rr + g, :].bitcast(FP8X4),
                        lhsT_scale=xs[:, rb + 2 * rr + g, :],
                        rhs=wc[:, r, g * 256:(g + 1) * 256].bitcast(FP8X4),
                        rhs_scale=ws[:, r, g * 256:(g + 1) * 256],
                        start=(g == 0),
                        stop=(g == 1),
                    )
            if q in MXS0:
                for rr in range(2):
                    r = 2 * jr + rr
                    for g in range(2):
                        nc.tensor.matmul_mx(
                            out=st[q]["s0"][:, j * 256:(j + 1) * 256],
                            lhsT=xc[:, rb + 2 * rr + g, :].bitcast(FP8X4),
                            lhsT_scale=xs[:, rb + 2 * rr + g, :],
                            rhs=wc[:, r, g * 256:(g + 1) * 256].bitcast(FP8X4),
                            rhs_scale=ws[:, r, g * 256:(g + 1) * 256],
                            start=(r == 0 and g == 0),
                            stop=(r == 7 and g == 1),
                        )
            nc.scalar.copy(out=u[:, j * 2048 + jr * 512: j * 2048 + (jr + 1) * 512], in_=ups[:])
            if q in S0_V:
                s1 = st[q]["s"]
                for rr in range(2):
                    nc.vector.scalar_tensor_tensor(
                        out=s1[:, j * 256:(j + 1) * 256], in0=ups[:, rr * 256:(rr + 1) * 256], scalar=1.0 / 16.0,
                        in1=(bc[:] if 2 * jr + rr == 0 else s1[:, j * 256:(j + 1) * 256]), op0=ALU.mult, op1=ALU.add,
                    )

        def s0_bias(q):
            d = st[q]
            nc.vector.scalar_tensor_tensor(
                out=d["s"][:].rearrange("p (j k) -> p j k", k=256), in0=d["s0"][:].rearrange("p (j k) -> p j k", k=256),
                scalar=1.0 / 16.0, in1=bc[:].unsqueeze(1).to_broadcast([P, d["nj"], 256]), op0=ALU.mult, op1=ALU.add,
            )

        def gr(q):
            return G_R if q >= G_FROM else 0

        def go(q, k):
            return G_O if q >= G_FROM and (k > 0 or not (q in S0_V or q in MXS0)) else 0

        def c_copy(q):
            d = st[q]
            d["cp"] = ps_sh.tile([P, P * d["nj"]], F32, tag="sh", name="cp")
            nc.tensor.matmul(out=d["cp"][:], lhsT=ident[:], rhs=d["td"][:], start=True, stop=True)

        def s_mult_g(q, j):
            d = st[q]
            n = gr(q)
            if j == 0:
                d["p"] = big.tile([P, 2048 * d["nj"]], F32, tag="big", name="p_s", align_bytes=64)
            pv = d["p"][:].rearrange("p (a o c) -> p a o c", o=16, c=16)
            uv = d["u"][:].rearrange("p (a o c) -> p a o c", o=16, c=16)
            cv = d["td"][:].rearrange("p (a c) -> p a c", c=16)
            nc.gpsimd.tensor_tensor(
                out=pv[:, 8 * j + 8 - n:8 * j + 8], in0=uv[:, 8 * j + 8 - n:8 * j + 8],
                in1=cv[:, 8 * j + 8 - n:8 * j + 8, :].unsqueeze(2).to_broadcast([P, n, 16, 16]), op=ALU.mult,
            )

        def s_copy(q):
            d = st[q]
            n = G_O
            d["sg"] = un.tile([P, 16 * n * d["nj"]], F32, tag="sg", name="sg")
            nc.scalar.copy(
                out=d["sg"][:].rearrange("p (j k) -> p j k", k=16 * n),
                in_=d["s"][:].rearrange("p (j k) -> p j k", k=256)[:, :, 256 - 16 * n:],
            )

        def a_half(q, j):
            pk = st[q]["pa"][:].rearrange("p (j o k) -> p j o k", o=16, k=P)
            nc.gpsimd.tensor_tensor(out=pk[:, j, 0:HA], in0=pk[:, j, 0:HA], in1=pk[:, j, 16 - HA:16], op=ALU.add)

        def s_half(q, j):
            pk = st[q]["p"][:].rearrange("p (j r k) -> p j r k", r=8, k=256)
            nc.gpsimd.tensor_tensor(out=pk[:, j, 0:HS], in0=pk[:, j, 0:HS], in1=pk[:, j, 8 - HS:8], op=ALU.add)

        def a_mult_g(q, j):
            d = st[q]
            n = G_O
            if j == 0:
                d["pa"] = big.tile([P, 2048 * d["nj"]], F32, tag="big", name="p_a", align_bytes=64)
            pv = d["pa"][:].rearrange("p (j o r c) -> p j o r c", o=16, r=8, c=16)
            uv = d["u"][:].rearrange("p (j r o c) -> p j o r c", r=8, o=16, c=16)
            sv = d["sg"][:].rearrange("p (j o c) -> p j o c", o=n, c=16)
            nc.gpsimd.tensor_tensor(
                out=pv[:, j, 16 - n:], in0=uv[:, j, 16 - n:],
                in1=sv[:, j].unsqueeze(2).to_broadcast([P, n, 8, 16]), op=ALU.mult,
            )

        turns = [0]

        def turn(dst, src, first, last, plain=False):
            turns[0] = turns[0] + 1
            nc.tensor.matmul(out=dst, lhsT=src, rhs=ident[:], is_transpose=not plain, start=first, stop=last)

        def acc_transposes(dst, srcs):
            n = len(srcs)
            for i in range(n):
                turn(dst, srcs[i], i == 0, i == n - 1)

        def s_mult(q, j):
            d = st[q]
            n = 8 - gr(q)
            if j == 0 and n == 8:
                d["p"] = big.tile([P, 2048 * d["nj"]], F32, tag="big", name="p_s", align_bytes=64)
            pv = d["p"][:].rearrange("p (a o c) -> p a o c", o=16, c=16)
            uv = d["u"][:].rearrange("p (a o c) -> p a o c", o=16, c=16)
            cv = (d["cp"] if gr(q) > 0 and C_PS else d["td"])[:].rearrange("p (a c) -> p a c", c=16)
            w = n // S_CUT
            for r in range(0, n, w):
                e = min(n, r + w)
                nc.vector.tensor_tensor(
                    out=pv[:, 8 * j + r:8 * j + e], in0=uv[:, 8 * j + r:8 * j + e],
                    in1=cv[:, 8 * j + r:8 * j + e, :].unsqueeze(2).to_broadcast([P, e - r, 16, 16]), op=ALU.mult,
                )

        def s_acc(q, k, j):
            d = st[q]
            src = d["u"] if k == 0 else d["p"]
            sv = src[:].rearrange("p (j r h k) -> p j r h k", r=8, h=2, k=P)
            if j == 0:
                d["acc"] = ps_sh.tile([P, d["nj"], 2, P], F32, tag="sh", name="acc_s")
            for h in range(2):
                acc_transposes(d["acc"][:, j, h, :], [sv[:, j, r, h, :] for r in range(8 - (HS if k > 0 and q in HU else 0))])

        def s_evac(q, k):
            d = st[q]
            d["ta"] = un.tile([P, 256 * d["nj"]], F32, tag="ta", name="ta")
            tv = d["ta"][:].rearrange("p (j h b) -> p j h b", h=2, b=P)
            for h in range(2):
                nc.scalar.activation(
                    out=tv[:, :, h, :], in_=d["acc"][:, :, h, :], func=ACT.Identity,
                    bias=bias_t[:, h:h + 1], scale=(1.0 / 16.0 if k == 0 else 1.0),
                )

        def s_back(q):
            d = st[q]
            d["s"] = ps_sh.tile([P, 256 * d["nj"]], F32, tag="sh", name="back_s")
            for jh in range(2 * d["nj"]):
                turn(d["s"][:, jh * P:(jh + 1) * P], d["ta"][:, jh * P:(jh + 1) * P], True, True, SB_PLAIN)

        def n2_pe(q, k):
            return N2_PE and (k > 0 or not (q in S0_V or q in MXS0))

        def sq_square(q, k):
            d = st[q]
            d["sq"] = un.tile([P, 256 * d["nj"]], F32, tag="sq", name="sq", bufs=3)
            src = d["ta"] if n2_pe(q, k) else d["s"]
            if G_SQ and k < 2 and q >= G_FROM and n2_pe(q, k):
                nc.gpsimd.tensor_tensor(out=d["sq"][:], in0=src[:], in1=src[:], op=ALU.mult)
            else:
                nc.scalar.activation(out=d["sq"][:], in_=src[:], func=ACT.Square)

        def sq_n2(q, k):
            d = st[q]
            if n2_pe(q, k):
                d["n2"] = ps_sh.tile([P, 16 * d["nj"]], F32, tag="sh", name="n2p")
                for jh in range(2 * d["nj"]):
                    nc.tensor.matmul(
                        out=d["n2"][:, (jh // 2) * 16:(jh // 2) * 16 + 16], lhsT=d["sq"][:, jh * P:(jh + 1) * P],
                        rhs=sel[:], start=(jh % 2 == 0), stop=(jh % 2 == 1),
                    )
            else:
                d["n2"] = un.tile([P, 16 * d["nj"]], F32, tag="n2", name="n2")
                nc.vector.tensor_reduce(
                    out=d["n2"][:].rearrange("p (j c) -> p j c", c=16),
                    in_=d["sq"][:].rearrange("p (j o c) -> p j c o", o=16, c=16),
                    axis=AX.X, op=ALU.add,
                )

        def sq_rd(q):
            d = st[q]
            d["rd"] = un.tile([P, 16 * d["nj"]], F32, tag="rd", name="rd")
            d["nn"] = un.tile([P, 16 * d["nj"]], F32, tag="nn", name="nn")
            if NN_FIRST:
                nc.scalar.activation(out=d["nn"][:], in_=d["n2"][:], func=ACT.Sqrt, bias=tinyb[:, 0:1])
            if RD_S:
                nc.scalar.activation(out=d["rd"][:], in_=d["n2"][:], func=ACT.Identity, bias=1.0 + EPS)
            else:
                nc.vector.tensor_scalar(out=d["rd"][:], in0=d["n2"][:], scalar1=1.0 + EPS, scalar2=None, op0=ALU.add)
            if not NN_FIRST:
                nc.scalar.activation(out=d["nn"][:], in_=d["n2"][:], func=ACT.Sqrt, bias=tinyb[:, 0:1])

        def sq_recip(q):
            d = st[q]
            nc.vector.reciprocal(out=d["rd"][:], in_=d["rd"][:])

        def sq_gain(q):
            d = st[q]
            d["gain"] = un.tile([P, 16 * d["nj"]], F32, tag="gain", name="gain")
            nc.vector.tensor_mul(out=d["gain"][:], in0=d["nn"][:], in1=d["rd"][:])

        def a_mult(q, k, j):
            d = st[q]
            n = 16 - go(q, k)
            if j == 0 and n == 16:
                d["pa"] = big.tile([P, 2048 * d["nj"]], F32, tag="big", name="p_a", align_bytes=64)
            pv = d["pa"][:].rearrange("p (j o r c) -> p j o r c", o=16, r=8, c=16)
            uv = d["u"][:].rearrange("p (j r o c) -> p j o r c", r=8, o=16, c=16)
            sv = d["s"][:].rearrange("p (j o c) -> p j o c", o=16, c=16)
            w = n // A_CUT
            for o in range(0, n, w):
                e = min(n, o + w)
                nc.vector.tensor_tensor(
                    out=pv[:, j, o:e], in0=uv[:, j, o:e],
                    in1=sv[:, j, o:e].unsqueeze(2).to_broadcast([P, e - o, 8, 16]), op=ALU.mult,
                )

        def a_acc(q, j):
            d = st[q]
            pk = d["pa"][:].rearrange("p (j o k) -> p j o k", o=16, k=P)
            if j == 0:
                d["acca"] = ps_sh.tile([P, d["nj"], P], F32, tag="sh", name="acc_a")
            acc_transposes(d["acca"][:, j, :], [pk[:, j, o, :] for o in range(16 - (HA if q in HU else 0))])

        def a_evac(q):
            d = st[q]
            d["tb"] = un.tile([P, P * d["nj"]], F32, tag="tb", name="tb")
            nc.scalar.copy(out=d["tb"][:].rearrange("p (j b) -> p j b", b=P), in_=d["acca"][:])

        def a_back(q):
            d = st[q]
            d["araw"] = ps_sh.tile([P, P * d["nj"]], F32, tag="sh", name="back_a")
            for j in range(d["nj"]):
                turn(d["araw"][:, j * P:(j + 1) * P], d["tb"][:, j * P:(j + 1) * P], True, True, AB_PLAIN)

        def a_logit(q, k):
            d = st[q]
            gv = d["gain"][:].rearrange("p (j c) -> p j c", c=16).unsqueeze(2).to_broadcast([P, d["nj"], 8, 16])
            av = d["araw"][:].rearrange("p (j r c) -> p j r c", r=8, c=16)
            if k == 0:
                d["logit"] = u_pool.tile([P, P * d["nj"]], F32, tag="logit%d" % q, name="logit")
                nc.vector.tensor_tensor(
                    out=d["logit"][:].rearrange("p (j r c) -> p j r c", r=8, c=16), in0=av, in1=gv, op=ALU.mult
                )
            else:
                tmp = d["tb"]
                nc.vector.tensor_tensor(
                    out=tmp[:].rearrange("p (j r c) -> p j r c", r=8, c=16), in0=av, in1=gv, op=ALU.mult
                )
                eng = nc.gpsimd if G_ADD and q >= G_FROM else nc.vector
                eng.tensor_tensor(out=d["logit"][:], in0=tmp[:], in1=d["logit"][:], op=ALU.add)

        def a_max(q):
            d = st[q]
            lv = d["logit"][:].rearrange("p (a c) -> p a c", c=16)
            d["mx"] = un.tile([P, 8 * d["nj"]], F32, tag="mx", name="mx")
            nc.vector.tensor_reduce(out=d["mx"][:], in_=lv, axis=AX.X, op=ALU.max)
            d["td"] = un.tile([P, P * d["nj"]], F32, tag="td", name="td")
            (nc.gpsimd if G_SUB and q >= G_FROM else nc.vector).tensor_tensor(
                out=d["td"][:].rearrange("p (a c) -> p a c", c=16), in0=lv,
                in1=d["mx"][:].unsqueeze(2).to_broadcast([P, 8 * d["nj"], 16]), op=ALU.subtract,
            )

        def a_exp(q):
            d = st[q]
            nc.scalar.activation(out=d["td"][:], in_=d["td"][:], func=ACT.Exp)

        def a_sum(q):
            d = st[q]
            ev = d["td"][:].rearrange("p (a c) -> p a c", c=16)
            nc.vector.tensor_reduce(out=d["mx"][:], in_=ev, axis=AX.X, op=ALU.add)

        def a_soft(q):
            d = st[q]
            ev = d["td"][:].rearrange("p (a c) -> p a c", c=16)
            nc.vector.reciprocal(out=d["mx"][:], in_=d["mx"][:])
            (nc.gpsimd if G_NORM and q >= G_FROM else nc.vector).tensor_tensor(
                out=ev, in0=ev, in1=d["mx"][:].unsqueeze(2).to_broadcast([P, 8 * d["nj"], 16]), op=ALU.mult
            )

        def out_v(q):
            d = st[q]
            nc.vector.tensor_tensor(
                out=d["ta"][:].rearrange("p (j c o) -> p j c o", c=16, o=16),
                in0=d["s"][:].rearrange("p (j o c) -> p j c o", o=16, c=16),
                in1=d["gain"][:].rearrange("p (j c) -> p j c", c=16).unsqueeze(3).to_broadcast([P, d["nj"], 16, 16]),
                op=ALU.mult,
            )
            nc.sync.dma_start(
                out=out[UNITS[q][0] * P:(UNITS[q][-1] + 1) * P].rearrange("(j b) c o -> b j (c o)", b=P),
                in_=d["ta"][:].rearrange("p (j k) -> p j k", k=256),
            )

        def end_evac(q, j):
            d = st[q]
            if j == 0:
                d["ta"] = un.tile([P, 256 * d["nj"]], F32, tag="ta", name="ta")
            tv = d["ta"][:].rearrange("p (j h b) -> p j h b", h=2, b=P)
            for h in range(2):
                nc.scalar.activation(
                    out=tv[:, j, h, :], in_=d["acc"][:, j, h, :], func=ACT.Identity, bias=bias_t[:, h:h + 1], scale=1.0
                )

        def end_back(q, j):
            d = st[q]
            if j == 0:
                d["s"] = ps_sh.tile([P, 256 * d["nj"]], F32, tag="sh", name="back_s")
                d["s1"] = ps_sh.tile([P, 256 * d["nj"]], F32, tag="sh", name="back_s1")
            dst = d["s"] if j == 0 else d["s1"]
            for h in range(2):
                turn(dst[:, h * P:(h + 1) * P], d["ta"][:, (2 * j + h) * P:(2 * j + h + 1) * P], True, True)

        def end_square(q, j):
            d = st[q]
            if j == 0:
                d["sq"] = un.tile([P, 256 * d["nj"]], F32, tag="sq", name="sq", bufs=3)
            nc.scalar.activation(out=d["sq"][:, j * 256:(j + 1) * 256], in_=d["ta"][:, j * 256:(j + 1) * 256], func=ACT.Square)

        def end_gain(q, j):
            d = st[q]
            n2 = ps_sh.tile([P, 16], F32, tag="sh", name="n2e")
            for h in range(2):
                nc.tensor.matmul(
                    out=n2[:], lhsT=d["sq"][:, (2 * j + h) * P:(2 * j + h + 1) * P], rhs=sel[:],
                    start=(h == 0), stop=(h == 1),
                )
            nn = un.tile([P, 32], F32, tag="nn", name="nne")
            rd = un.tile([P, 32], F32, tag="rd", name="rde")
            gain = un.tile([P, 32], F32, tag="gain", name="gaine")
            nc.scalar.activation(out=nn[:, 0:16], in_=n2[:], func=ACT.Sqrt, bias=tinyb[:, 0:1])
            nc.vector.tensor_scalar(out=rd[:, 0:16], in0=n2[:], scalar1=1.0 + EPS, scalar2=None, op0=ALU.add)
            nc.vector.reciprocal(out=rd[:, 0:16], in_=rd[:, 0:16])
            nc.vector.tensor_mul(out=gain[:, 0:16], in0=nn[:, 0:16], in1=rd[:, 0:16])
            d["g%d" % j] = gain

        def end_out(q, j):
            d = st[q]
            src = d["s"] if j == 0 else d["s1"]
            nc.vector.tensor_tensor(
                out=d["ta"][:, j * 256:(j + 1) * 256].rearrange("p (c o) -> p c o", o=16),
                in0=src[:, 0:256].rearrange("p (o c) -> p c o", c=16),
                in1=d["g%d" % j][:, 0:16].unsqueeze(2).to_broadcast([P, 16, 16]), op=ALU.mult,
            )
            nc.sync.dma_start(
                out=out[UNITS[q][j] * P:(UNITS[q][j] + 1) * P].rearrange("b c o -> b (c o)"),
                in_=d["ta"][:, j * 256:(j + 1) * 256],
            )

        def routing_steps(q):
            steps = []
            js = range(st[q]["nj"])

            def add(*fs, w=None, n="x"):
                for f in fs:
                    steps.append((f, WN.get(n, WS if w is None else w)))

            for k in range(3):
                if k == 0 and q in MXS0:
                    add(lambda: s0_bias(q), n="s0b")
                if k > 0:
                    if gr(q) > 0:
                        add(*[lambda j=j: s_mult_g(q, j) for j in js], w=WG, n="smg")
                        if C_PS:
                            add(lambda: c_copy(q), n="cc")
                    add(*[lambda j=j: s_mult(q, j) for j in js], w=WM, n="sm")
                    if HS > 0 and q in HU:
                        add(*[lambda j=j: s_half(q, j) for j in js], w=WG, n="sh")
                if k == 2 and q in SPLIT_END:
                    ends = [
                        lambda j: s_acc(q, 2, j),
                        lambda j: end_evac(q, j),
                        lambda j: (end_square(q, j), end_back(q, j)),
                        lambda j: end_gain(q, j),
                        lambda j: end_out(q, j),
                    ]
                    for i in range(5 + 2 * (len(js) - 1)):
                        for j in js:
                            if 0 <= i - 2 * j < 5:
                                add(lambda f=ends[i - 2 * j], j=j: f(j), w=WE)
                    continue
                if k > 0 or not (q in S0_V or q in MXS0):
                    add(*[lambda j=j, k=k: s_acc(q, k, j) for j in js], w=WA, n="sa")
                    add(lambda k=k: s_evac(q, k), n="se")
                    add(lambda: s_back(q), n="sb")
                add(lambda k=k: sq_square(q, k), n="sq")
                if k < 2:
                    if go(q, k) > 0:
                        add(lambda: s_copy(q), n="sc")
                        add(*[lambda j=j: a_mult_g(q, j) for j in js], w=WG, n="amg")
                    add(lambda k=k: a_mult(q, k, 0), w=WM, n="am")
                    add(lambda k=k: sq_n2(q, k), n="n2")
                    add(*[lambda j=j, k=k: a_mult(q, k, j) for j in js if j > 0], w=WM, n="am")
                    if HA > 0 and q in HU:
                        add(*[lambda j=j: a_half(q, j) for j in js], w=WG, n="ah")
                    add(lambda: a_acc(q, 0), w=WA, n="aa")
                    add(lambda: sq_rd(q), n="rd")
                    add(*[lambda j=j: a_acc(q, j) for j in js if j > 0], w=WA, n="aa")
                    if SPL_GA:
                        add(lambda: sq_recip(q), n="ga")
                        add(lambda: (a_evac(q), sq_gain(q)), n="ae")
                    else:
                        add(lambda: (sq_recip(q), sq_gain(q)), n="ga")
                        add(lambda: a_evac(q), n="ae")
                    add(lambda: a_back(q), n="ab")
                    if SPL_LO:
                        add(lambda k=k: a_logit(q, k), n="lo", w=WL)
                        add(lambda: a_max(q), n="mx")
                    else:
                        add(lambda k=k: (a_logit(q, k), a_max(q)), n="lo")
                    add(lambda: a_exp(q), n="ex")
                    if SPL_SO:
                        add(lambda: a_sum(q), n="so", w=WL)
                        add(lambda: a_soft(q), n="so2")
                    else:
                        add(lambda: (a_sum(q), a_soft(q)), n="so")
                else:
                    add(lambda k=k: sq_n2(q, k), n="n2")
                    add(lambda: sq_rd(q), n="rd")
                    add(lambda: (sq_recip(q), sq_gain(q)), n="ga")
                    add(lambda: out_v(q), n="ov")
            return steps

        chains = []

        def advance(n, boost=0.0):
            for rep in range(n):
                for ch in (chains if OLD_FIRST else chains[::-1]):
                    ch[2] = ch[2] + 1.0 + boost * ch[3]
                    while ch[1] < len(ch[0]) and ch[2] >= 0.999:
                        ch[0][ch[1]][0]()
                        ch[2] = ch[2] - ch[0][ch[1]][1]
                        ch[1] = ch[1] + 1

        load_w(0)
        load_x(0, 0)
        load_w(1)
        load_x(0, 1)
        load_w(2)
        load_bias()
        load_w(3)
        load_x(1, 0)
        load_x(1, 1)
        if MANUAL:
            ctx.enter_context(tc.manual_schedule())
        owed = [0.0]

        def pace(i):
            owed[0] = owed[0] + (RATE if i < 32 else LATE_RATE)
            while owed[0] >= 1.0:
                owed[0] = owed[0] - 1.0
                advance(1, FBOOST)

        for i in range(32 + MX_LAG):
            for o in ORDER:
                if o == "T" and i < 32:
                    if i % 4 == 0 and 2 <= i // 4 + 1 < 8:
                        load_x(i // 4 + 1, 0)
                        load_x(i // 4 + 1, 1)
                    if i < 4:
                        w_step(i)
                    if i == 2:
                        prep_bias()
                    fe_transposes(i)
                if o == "Q":
                    if i < 4:
                        w_quant(i)
                    if 0 <= i - 1 < 32:
                        fe_quant(i - 1)
                if o == "M" and i >= MX_LAG and (i - MX_LAG) % MX_GRP == MX_GRP - 1:
                    for b in range(i - MX_LAG - MX_GRP + 1, i - MX_LAG + 1):
                        fe_mx(b)
                    t = (i - MX_LAG) // 4
                    q = unit_of[t][0]
                    if (i - MX_LAG) % 4 == 3 and t == UNITS[q][-1]:
                        chains.append([routing_steps(q), 0, 0.0, q])
                if o == "A":
                    pace(i)
        for rep in range(TAIL):
            advance(1, BOOST)
